import numpy as np
import ml_dtypes


def mxq(x, axis, fmt="e4m3"):
    dtype, down = {"e4m3": (ml_dtypes.float8_e4m3fn, 7), "e5m2": (ml_dtypes.float8_e5m2, 14)}[fmt]
    v = np.moveaxis(np.asarray(x, np.float32).astype(ml_dtypes.bfloat16).astype(np.float64), axis, -1)
    blocks = v.reshape(v.shape[:-1] + (-1, 32))
    amax = np.abs(blocks).max(-1, keepdims=True)
    byte = np.maximum(np.where(amax > 0, np.frexp(amax)[1] - 1 + 127, 0) - down, 1)
    scale = np.exp2(byte - 127.0)
    codes = (blocks / scale).astype(np.float32).astype(dtype).astype(np.float64)
    return np.moveaxis((codes * scale).reshape(v.shape), -1, axis)


WIDE = False


def mx_kscale(k):
    if not WIDE:
        return np.ones(k)
    levels = np.array([10, -10, 5, -5, 0])
    if k % 512:
        return np.exp2(np.random.permutation(np.resize(levels, k // 32))).repeat(32)
    a = np.empty((k // 512, 16))
    for p in range(k // 512):
        a[p, :8] = np.random.permutation(np.resize(levels, 8))
        for g in range(8):
            far = levels[np.abs(levels - a[p, g]) >= 10]
            a[p, g + 8] = far[np.random.randint(len(far))]
    return np.exp2(a.ravel()).repeat(32)


BF16 = ml_dtypes.bfloat16


def bf(x):
    return np.asarray(x, np.float32).astype(BF16)


def f64(x):
    return np.asarray(x).astype(np.float64)


B, S, DIM, H, HD = 4, 128, 2048, 16, 128
HALF = HD // 2


def apply_rope(t, cos, sin):
    t1, t2 = t[..., :HALF], t[..., HALF:]
    c = cos[None, None, :t.shape[2], :HALF]
    s = sin[None, None, :t.shape[2], :HALF]
    return np.concatenate([t1 * c - t2 * s, t2 * c + t1 * s], axis=-1)


def draw0():
    s = mx_kscale(DIM)
    w = 1.0 / np.sqrt(DIM)
    return {"x": bf(np.random.standard_normal((B, S, DIM)) * s),
            "cos": bf(np.random.uniform(size=(S, HALF))),
            "sin": bf(np.random.uniform(size=(S, HALF))),
            "wq": bf(np.random.standard_normal((DIM, H * HD)) * w / s[:, None]),
            "wk": bf(np.random.standard_normal((DIM, H * HD)) * w / s[:, None])}


def core(x, cos, sin, wq, wk):
    xq = mxq(f64(x), 2, "e4m3")
    q = (xq @ mxq(f64(wq), 0, "e4m3")).reshape(B, S, H, HD).transpose(0, 2, 1, 3)
    k = (xq @ mxq(f64(wk), 0, "e4m3")).reshape(B, S, H, HD).transpose(0, 2, 1, 3)
    return apply_rope(q, f64(cos), f64(sin)), apply_rope(k, f64(cos), f64(sin))


def e4m3fn_bytes(y):
    return np.clip(np.asarray(y, np.float64), -448.0, 448.0).astype(np.float32).astype(ml_dtypes.float8_e4m3fn).view(np.uint8)


def e4m3fn_values(b):
    return np.asarray(b, np.uint8).view(ml_dtypes.float8_e4m3fn).astype(np.float64)


def setup_inputs():
    d = draw0()
    x0 = np.asarray(d['wq']).astype(np.float64)
    s = (np.max(np.abs(x0), axis=(1,), keepdims=True) / 448.0).astype(np.float32)
    out = {}
    for k, v in d.items():
        if k == 'wq':
            out['wq_bytes'] = e4m3fn_bytes(x0 / s.astype(np.float64))
            out['wq_scale'] = s
        else:
            out[k] = v
    return out


def reference(x, cos, sin, wq_bytes, wq_scale, wk):
    return core(x, cos, sin, e4m3fn_values(wq_bytes) * wq_scale.astype(np.float64), wk)

@@ -1,0 +1,186 @@
+from contextlib import ExitStack
+
+import concourse.masks as masks
+import concourse.mybir as mybir
+
+F32 = mybir.dt.float32
+BF16 = mybir.dt.bfloat16
+U32 = mybir.dt.uint32
+U8 = mybir.dt.uint8
+FP8 = mybir.dt.float8_e4m3fn
+FP8X4 = mybir.dt.float8_e4m3fn_x4
+ACT = mybir.ActivationFunctionType
+ALU = mybir.AluOpType
+
+BATCH, SEQ, DIM, HEADS, HEAD_DIM = 4, 128, 2048, 16, 128
+HALF = HEAD_DIM // 2
+P = 128
+PACK = 4
+K_PASS = P * PACK
+PASSES = DIM // K_PASS
+CHUNK = 512
+CHUNK_HEADS = CHUNK // HEAD_DIM
+BLOCKS = HEADS * HEAD_DIM // CHUNK
+
+FLOPS = 2 * BATCH * SEQ * DIM * 2 * HEADS * HEAD_DIM
+
+V_UNITS_OF_WK = (4, 4, 3, 3)
+MANUAL = False
+
+
+def tile_attention_pa_kernel(tc, x, cos, sin, wq_bytes, wq_scale, wk, out_0, out_1):
+    nc = tc.nc
+    with ExitStack() as ctx:
+        keep = ctx.enter_context(tc.tile_pool(name="keep", bufs=1))
+        xg_pool = ctx.enter_context(tc.tile_pool(name="xg", bufs=2))
+        wide_pool = ctx.enter_context(tc.tile_pool(name="wide", bufs=3))
+        grp_pool = ctx.enter_context(tc.tile_pool(name="grp", bufs=4))
+        code_pool = ctx.enter_context(tc.tile_pool(name="code", bufs=3))
+        epi_pool = ctx.enter_context(tc.tile_pool(name="epi", bufs=2))
+        psum = ctx.enter_context(tc.psum_pool(name="psum", bufs=8))
+        if MANUAL:
+            ctx.enter_context(tc.manual_schedule())
+
+        wq_rows = wq_bytes.rearrange("(g p t) n -> g p t n", p=P, t=PACK)
+        wk_rows = wk.rearrange("(g p t) n -> g p t n", p=P, t=PACK)
+        wq_raw = {}
+        wk_raw = {}
+
+        def load_block(blk):
+            cols = slice(blk * CHUNK, (blk + 1) * CHUNK)
+            for g in range(PASSES):
+                qb = keep.tile([P, PACK, CHUNK], U8, name="wq_bytes_%d_%d" % (blk, g))
+                nc.sync.dma_start(out=qb[:], in_=wq_rows[g, :, :, cols])
+                wq_raw[(blk, g)] = qb
+                kb = keep.tile([P, PACK, CHUNK], BF16, name="wk_raw_%d_%d" % (blk, g))
+                nc.sync.dma_start(out=kb[:], in_=wk_rows[g, :, :, cols])
+                wk_raw[(blk, g)] = kb
+
+        wq_scl = keep.tile([P, PASSES, PACK], F32, name="wq_scl")
+        nc.sync.dma_start(out=wq_scl[:], in_=wq_scale.rearrange("(g p t) o -> p g (t o)", p=P, t=PACK))
+        load_block(0)
+        x_raw = epi_pool.tile([P, BATCH, DIM], BF16, name="x_raw", tag="prod")
+        for b in range(BATCH):
+            nc.sync.dma_start(out=x_raw[:, b, :], in_=x[b])
+        cos_sin = keep.tile([P, 2, HALF], BF16, name="cos_sin")
+        nc.sync.dma_start(out=cos_sin[:, 0, :], in_=cos)
+        nc.sync.dma_start(out=cos_sin[:, 1, :], in_=sin)
+        for blk in range(1, BLOCKS):
+            load_block(blk)
+
+        ident = keep.tile([P, P], F32, name="ident")
+        masks.make_identity(nc, ident[:])
+        table = keep.tile([P, 2, CHUNK_HEADS, 2, HALF], F32, name="table")
+        for h in range(CHUNK_HEADS):
+            for u in range(2):
+                nc.gpsimd.tensor_copy(out=table[:, 0, h, u, :], in_=cos_sin[:, 0, :])
+            nc.gpsimd.tensor_copy(out=table[:, 1, h, 0, :], in_=cos_sin[:, 1, :])
+            nc.gpsimd.tensor_scalar(out=table[:, 1, h, 1, :], in0=cos_sin[:, 1, :], scalar1=-1.0, scalar2=None, op0=ALU.mult)
+
+        x_codes = keep.tile([P, BATCH, PASSES * P], U32, name="x_codes", align_bytes=64)
+        x_scales = keep.tile([P, BATCH, PASSES * P], U8, name="x_scales", align_bytes=64)
+
+        def prepare_x(b):
+            words = x_raw[:, b, :].bitcast(F32)
+            xg = xg_pool.tile([P, PASSES * P * PACK], BF16, name="x_grouped", align_bytes=64)
+            xg_words = xg[:].bitcast(F32).rearrange("p (g r u) -> p g r u", g=PASSES, u=2)
+            for half in range(2):
+                bank = psum.tile([P, 2, 2, P], F32, name="bank")
+                for gg in range(2):
+                    g = 2 * half + gg
+                    for u in range(2):
+                        nc.tensor.transpose(bank[:, gg, u, :], words[:, 256 * g + u : 256 * (g + 1) : 2], ident[:])
+                nc.scalar.copy(out=xg_words[:, 2 * half : 2 * half + 2, :, :], in_=bank[:].rearrange("p g u r -> p g r u"))
+            nc.vector.quantize_mx(out=x_codes[:, b, :].bitcast(FP8X4), scales=x_scales[:, b, :], in_=xg[:])
+
+        def widen(blk, g):
+            wide = wide_pool.tile([P, PACK, CHUNK], BF16, name="wq_wide")
+            for t in range(PACK):
+                nc.scalar.activation(
+                    out=wide[:, t, :],
+                    in_=wq_raw[(blk, g)][:, t, :].bitcast(FP8),
+                    func=ACT.Copy,
+                    scale=wq_scl[:, g, t : t + 1],
+                )
+            return wide
+
+        def new_grouped():
+            grouped = grp_pool.tile([P, 2, CHUNK, PACK], BF16, name="w_grouped", align_bytes=64)
+            return grouped
+
+        def interleave(on_vector, src, dst):
+            if on_vector:
+                nc.vector.tensor_copy(out=dst, in_=src[:].rearrange("p t c -> p c t"))
+            else:
+                nc.scalar.copy(out=dst, in_=src[:].rearrange("p t c -> p c t"))
+
+        def new_codes():
+            codes = code_pool.tile([P, PASSES, CHUNK], U32, name="w_codes", align_bytes=64)
+            scales = code_pool.tile([P, PASSES, CHUNK], U8, name="w_scales", align_bytes=64)
+            return codes, scales
+
+        def quantize(grouped, cs, g):
+            nc.vector.quantize_mx(
+                out=cs[0][:, g : g + 2, :].rearrange("p g c -> p (g c)").bitcast(FP8X4),
+                scales=cs[1][:, g : g + 2, :].rearrange("p g c -> p (g c)"),
+                in_=grouped[:].rearrange("p g c t -> p (g c t)"),
+            )
+
+        def project_and_rotate(cs, out_dram, blk, fine):
+            prod = epi_pool.tile([P, BATCH, 2, CHUNK_HEADS, 2, HALF], F32, name="prod", tag="prod")
+
+            def add_and_store(b0, b1):
+                for u in range(2):
+                    nc.vector.tensor_tensor(
+                        out=prod[:, b0:b1, 0, :, u, :],
+                        in0=prod[:, b0:b1, 0, :, u, :],
+                        in1=prod[:, b0:b1, 1, :, 1 - u, :],
+                        op=ALU.add,
+                    )
+                for b in range(b0, b1):
+                    nc.sync.dma_start(
+                        out=out_dram[b, blk * CHUNK_HEADS : (blk + 1) * CHUNK_HEADS].rearrange("h p d -> p h d"),
+                        in_=prod[:, b, 0].rearrange("p h u d -> p h (u d)"),
+                    )
+
+            for b in range(BATCH):
+                acc = psum.tile([P, CHUNK], F32, name="bank")
+                for g in range(PASSES):
+                    rows = slice(g * P, (g + 1) * P)
+                    nc.tensor.matmul_mx(
+                        out=acc[:],
+                        lhsT=x_codes[:, b, rows].bitcast(FP8X4),
+                        lhsT_scale=x_scales[:, b, rows],
+                        rhs=cs[0][:, g, :].bitcast(FP8X4),
+                        rhs_scale=cs[1][:, g, :],
+                        start=(g == 0),
+                        stop=(g == PASSES - 1),
+                    )
+                nc.vector.tensor_tensor(
+                    out=prod[:, b].rearrange("p r h u d -> p r (h u d)"),
+                    in0=acc[:].unsqueeze(1).to_broadcast([P, 2, CHUNK]),
+                    in1=table[:].rearrange("p r h u d -> p r (h u d)"),
+                    op=ALU.mult,
+                )
+                if fine:
+                    add_and_store(b, b + 1)
+            if not fine:
+                add_and_store(0, BATCH)
+
+        for blk in range(BLOCKS):
+            k_cs = new_codes()
+            q_cs = new_codes()
+            for g in range(0, PASSES, 2):
+                k_grouped = new_grouped()
+                q_grouped = new_grouped()
+                for j in range(2):
+                    wide = widen(blk, g + j)
+                    interleave(g + j < V_UNITS_OF_WK[blk], wk_raw[(blk, g + j)], k_grouped[:, j])
+                    interleave(False, wide, q_grouped[:, j])
+                quantize(k_grouped, k_cs, g)
+                quantize(q_grouped, q_cs, g)
+            if blk == 0:
+                for b in range(BATCH):
+                    prepare_x(b)
+            project_and_rotate(k_cs, out_1, blk, False)
+            project_and_rotate(q_cs, out_0, blk, blk == BLOCKS - 1)

@@ -24,7 +24,8 @@ BLOCKS = HEADS * HEAD_DIM // CHUNK
 
 FLOPS = 2 * BATCH * SEQ * DIM * 2 * HEADS * HEAD_DIM
 
-V_UNITS_OF_WK = (4, 4, 3, 3)
+WK_ROUTE = ("VVVV", "VVVV", "VVVT", "VVVT")
+WQ_ROUTE = ("TTTS", "TTTS", "TTSS", "TTSS")
 MANUAL = False
 
 
@@ -37,7 +38,8 @@ def tile_attention_pa_kernel(tc, x, cos, sin, wq_bytes, wq_scale, wk, out_0, out
         grp_pool = ctx.enter_context(tc.tile_pool(name="grp", bufs=4))
         code_pool = ctx.enter_context(tc.tile_pool(name="code", bufs=3))
         epi_pool = ctx.enter_context(tc.tile_pool(name="epi", bufs=2))
-        psum = ctx.enter_context(tc.psum_pool(name="psum", bufs=8))
+        psum = ctx.enter_context(tc.psum_pool(name="psum", bufs=6))
+        il_psum = ctx.enter_context(tc.psum_pool(name="il_psum", bufs=2))
         if MANUAL:
             ctx.enter_context(tc.manual_schedule())
 
@@ -70,6 +72,8 @@ def tile_attention_pa_kernel(tc, x, cos, sin, wq_bytes, wq_scale, wk, out_0, out
 
         ident = keep.tile([P, P], F32, name="ident")
         masks.make_identity(nc, ident[:])
+        ident_bf = keep.tile([P, P], BF16, name="ident_bf")
+        masks.make_identity(nc, ident_bf[:])
         table = keep.tile([P, 2, CHUNK_HEADS, 2, HALF], F32, name="table")
         for h in range(CHUNK_HEADS):
             for u in range(2):
@@ -108,11 +112,27 @@ def tile_attention_pa_kernel(tc, x, cos, sin, wq_bytes, wq_scale, wk, out_0, out
             grouped = grp_pool.tile([P, 2, CHUNK, PACK], BF16, name="w_grouped", align_bytes=64)
             return grouped
 
-        def interleave(on_vector, src, dst):
-            if on_vector:
-                nc.vector.tensor_copy(out=dst, in_=src[:].rearrange("p t c -> p c t"))
+        def interleave(route, src, dst):
+            if route == "T":
+                for half in range(2):
+                    il_bank = il_psum.tile([P, 2 * P, PACK], BF16, name="il_bank")
+                    for s in range(2):
+                        c0 = (2 * half + s) * P
+                        nc.tensor.matmul(
+                            out=il_bank[:, s * P : (s + 1) * P, :],
+                            lhsT=ident_bf[:],
+                            rhs=src[:, :, c0 : c0 + P].rearrange("p t c -> p c t"),
+                            start=True,
+                            stop=True,
+                        )
+                    nc.scalar.copy(out=dst[:, 2 * half * P : 2 * (half + 1) * P, :], in_=il_bank[:])
+                return
+            dst_view = dst.rearrange("p (c i) t -> p c t i", i=4)
+            src_view = src[:].rearrange("p t (c i) -> p c t i", i=4)
+            if route == "V":
+                nc.vector.tensor_copy(out=dst_view, in_=src_view)
             else:
-                nc.scalar.copy(out=dst, in_=src[:].rearrange("p t c -> p c t"))
+                nc.scalar.copy(out=dst_view, in_=src_view)
 
         def new_codes():
             codes = code_pool.tile([P, PASSES, CHUNK], U32, name="w_codes", align_bytes=64)
@@ -175,8 +195,8 @@ def tile_attention_pa_kernel(tc, x, cos, sin, wq_bytes, wq_scale, wk, out_0, out
                 q_grouped = new_grouped()
                 for j in range(2):
                     wide = widen(blk, g + j)
-                    interleave(g + j < V_UNITS_OF_WK[blk], wk_raw[(blk, g + j)], k_grouped[:, j])
-                    interleave(False, wide, q_grouped[:, j])
+                    interleave(WK_ROUTE[blk][g + j], wk_raw[(blk, g + j)], k_grouped[:, j])
+                    interleave(WQ_ROUTE[blk][g + j], wide, q_grouped[:, j])
                 quantize(k_grouped, k_cs, g)
                 quantize(q_grouped, q_cs, g)
             if blk == 0:

@@ -24,78 +24,112 @@ BLOCKS = HEADS * HEAD_DIM // CHUNK
 
 FLOPS = 2 * BATCH * SEQ * DIM * 2 * HEADS * HEAD_DIM
 
-WK_ROUTE = ("VVVV", "VVVV", "VVVT", "VVVT")
-WQ_ROUTE = ("TTTS", "TTTS", "TTSS", "TTSS")
-MANUAL = False
+G_BANKS_OF_8 = 5
+G_BANKS_OF_4 = 2
 
 
 def tile_attention_pa_kernel(tc, x, cos, sin, wq_bytes, wq_scale, wk, out_0, out_1):
     nc = tc.nc
     with ExitStack() as ctx:
         keep = ctx.enter_context(tc.tile_pool(name="keep", bufs=1))
+        raw_pool = ctx.enter_context(tc.tile_pool(name="raw", bufs=3))
         xg_pool = ctx.enter_context(tc.tile_pool(name="xg", bufs=2))
         wide_pool = ctx.enter_context(tc.tile_pool(name="wide", bufs=3))
-        grp_pool = ctx.enter_context(tc.tile_pool(name="grp", bufs=4))
+        kgrp_pool = ctx.enter_context(tc.tile_pool(name="kgrp", bufs=2))
+        qgrp_pool = ctx.enter_context(tc.tile_pool(name="qgrp", bufs=4))
         code_pool = ctx.enter_context(tc.tile_pool(name="code", bufs=3))
         epi_pool = ctx.enter_context(tc.tile_pool(name="epi", bufs=2))
-        psum = ctx.enter_context(tc.psum_pool(name="psum", bufs=6))
-        il_psum = ctx.enter_context(tc.psum_pool(name="il_psum", bufs=2))
-        if MANUAL:
-            ctx.enter_context(tc.manual_schedule())
+        psum = ctx.enter_context(tc.psum_pool(name="psum", bufs=8))
+        ctx.enter_context(tc.manual_schedule())
 
         wq_rows = wq_bytes.rearrange("(g p t) n -> g p t n", p=P, t=PACK)
         wk_rows = wk.rearrange("(g p t) n -> g p t n", p=P, t=PACK)
         wq_raw = {}
         wk_raw = {}
 
-        def load_block(blk):
-            cols = slice(blk * CHUNK, (blk + 1) * CHUNK)
-            for g in range(PASSES):
-                qb = keep.tile([P, PACK, CHUNK], U8, name="wq_bytes_%d_%d" % (blk, g))
-                nc.sync.dma_start(out=qb[:], in_=wq_rows[g, :, :, cols])
-                wq_raw[(blk, g)] = qb
-                kb = keep.tile([P, PACK, CHUNK], BF16, name="wk_raw_%d_%d" % (blk, g))
-                nc.sync.dma_start(out=kb[:], in_=wk_rows[g, :, :, cols])
-                wk_raw[(blk, g)] = kb
+        def load_wq(blk, g):
+            qb = raw_pool.tile([P, PACK, CHUNK], U8, name="wq_bytes_%d" % g)
+            nc.sync.dma_start(out=qb[:], in_=wq_rows[g, :, :, blk * CHUNK : (blk + 1) * CHUNK])
+            wq_raw[(blk, g)] = qb
 
-        wq_scl = keep.tile([P, PASSES, PACK], F32, name="wq_scl")
-        nc.sync.dma_start(out=wq_scl[:], in_=wq_scale.rearrange("(g p t) o -> p g (t o)", p=P, t=PACK))
-        load_block(0)
-        x_raw = epi_pool.tile([P, BATCH, DIM], BF16, name="x_raw", tag="prod")
-        for b in range(BATCH):
-            nc.sync.dma_start(out=x_raw[:, b, :], in_=x[b])
+        def load_wk(blk, g):
+            kb = raw_pool.tile([P, PACK, CHUNK], BF16, name="wk_raw_%d" % g)
+            nc.sync.dma_start(out=kb[:], in_=wk_rows[g, :, :, blk * CHUNK : (blk + 1) * CHUNK])
+            wk_raw[(blk, g)] = kb
+
         cos_sin = keep.tile([P, 2, HALF], BF16, name="cos_sin")
         nc.sync.dma_start(out=cos_sin[:, 0, :], in_=cos)
         nc.sync.dma_start(out=cos_sin[:, 1, :], in_=sin)
-        for blk in range(1, BLOCKS):
-            load_block(blk)
+        wq_scl = keep.tile([P, PASSES, PACK], F32, name="wq_scl")
+        nc.sync.dma_start(out=wq_scl[:], in_=wq_scale.rearrange("(g p t) o -> p g (t o)", p=P, t=PACK))
+        for g in range(PASSES):
+            load_wq(0, g)
+            load_wk(0, g)
+        x_raw = epi_pool.tile([P, BATCH, DIM], BF16, name="x_raw", tag="prod")
+        nc.sync.dma_start(out=x_raw[:, 0, :], in_=x[0])
+        nc.sync.dma_start(out=x_raw[:, 1, :], in_=x[1])
+        load_wk(1, 0)
+        nc.sync.dma_start(out=x_raw[:, 2, :], in_=x[2])
+        load_wk(1, 1)
+        nc.sync.dma_start(out=x_raw[:, 3, :], in_=x[3])
+        load_wk(1, 2)
+        load_wk(1, 3)
+        for g in range(PASSES):
+            load_wq(1, g)
+        for g in range(PASSES):
+            load_wk(2, g)
+        for g in range(PASSES):
+            load_wq(2, g)
 
         ident = keep.tile([P, P], F32, name="ident")
         masks.make_identity(nc, ident[:])
-        ident_bf = keep.tile([P, P], BF16, name="ident_bf")
-        masks.make_identity(nc, ident_bf[:])
         table = keep.tile([P, 2, CHUNK_HEADS, 2, HALF], F32, name="table")
-        for h in range(CHUNK_HEADS):
-            for u in range(2):
-                nc.gpsimd.tensor_copy(out=table[:, 0, h, u, :], in_=cos_sin[:, 0, :])
-            nc.gpsimd.tensor_copy(out=table[:, 1, h, 0, :], in_=cos_sin[:, 1, :])
-            nc.gpsimd.tensor_scalar(out=table[:, 1, h, 1, :], in0=cos_sin[:, 1, :], scalar1=-1.0, scalar2=None, op0=ALU.mult)
+        nc.gpsimd.tensor_scalar(
+            out=table[:, 0].rearrange("p h u d -> p (h u) d"),
+            in0=cos_sin[:, 0, :].unsqueeze(1).to_broadcast([P, 2 * CHUNK_HEADS, HALF]),
+            scalar1=1.0,
+            scalar2=0.0,
+            op0=ALU.mult,
+            op1=ALU.add,
+        )
+        for u in range(2):
+            nc.gpsimd.tensor_scalar(
+                out=table[:, 1, :, u, :],
+                in0=cos_sin[:, 1, :].unsqueeze(1).to_broadcast([P, CHUNK_HEADS, HALF]),
+                scalar1=1.0 - 2.0 * u,
+                scalar2=0.0,
+                op0=ALU.mult,
+                op1=ALU.add,
+            )
 
         x_codes = keep.tile([P, BATCH, PASSES * P], U32, name="x_codes", align_bytes=64)
         x_scales = keep.tile([P, BATCH, PASSES * P], U8, name="x_scales", align_bytes=64)
 
-        def prepare_x(b):
+        def transpose_x(b):
             words = x_raw[:, b, :].bitcast(F32)
-            xg = xg_pool.tile([P, PASSES * P * PACK], BF16, name="x_grouped", align_bytes=64)
-            xg_words = xg[:].bitcast(F32).rearrange("p (g r u) -> p g r u", g=PASSES, u=2)
+            banks = []
             for half in range(2):
                 bank = psum.tile([P, 2, 2, P], F32, name="bank")
                 for gg in range(2):
                     g = 2 * half + gg
                     for u in range(2):
                         nc.tensor.transpose(bank[:, gg, u, :], words[:, 256 * g + u : 256 * (g + 1) : 2], ident[:])
-                nc.scalar.copy(out=xg_words[:, 2 * half : 2 * half + 2, :, :], in_=bank[:].rearrange("p g u r -> p g r u"))
-            nc.vector.quantize_mx(out=x_codes[:, b, :].bitcast(FP8X4), scales=x_scales[:, b, :], in_=xg[:])
+                banks.append(bank)
+            return banks
+
+        def empty_x(banks, xg, j):
+            xg_words = xg[:, j, :].bitcast(F32).rearrange("p (g r u) -> p g r u", g=PASSES, u=2)
+            for half in range(2):
+                nc.scalar.copy(
+                    out=xg_words[:, 2 * half : 2 * half + 2, :, :], in_=banks[half][:].rearrange("p g u r -> p g r u")
+                )
+
+        def quantize_x(xg, b):
+            nc.vector.quantize_mx(
+                out=x_codes[:, b : b + 2, :].rearrange("p b c -> p (b c)").bitcast(FP8X4),
+                scales=x_scales[:, b : b + 2, :].rearrange("p b c -> p (b c)"),
+                in_=xg[:].rearrange("p b c -> p (b c)"),
+            )
 
         def widen(blk, g):
             wide = wide_pool.tile([P, PACK, CHUNK], BF16, name="wq_wide")
@@ -108,61 +142,41 @@ def tile_attention_pa_kernel(tc, x, cos, sin, wq_bytes, wq_scale, wk, out_0, out
                 )
             return wide
 
-        def new_grouped():
-            grouped = grp_pool.tile([P, 2, CHUNK, PACK], BF16, name="w_grouped", align_bytes=64)
-            return grouped
-
-        def interleave(route, src, dst):
-            if route == "T":
-                for half in range(2):
-                    il_bank = il_psum.tile([P, 2 * P, PACK], BF16, name="il_bank")
-                    for s in range(2):
-                        c0 = (2 * half + s) * P
-                        nc.tensor.matmul(
-                            out=il_bank[:, s * P : (s + 1) * P, :],
-                            lhsT=ident_bf[:],
-                            rhs=src[:, :, c0 : c0 + P].rearrange("p t c -> p c t"),
-                            start=True,
-                            stop=True,
-                        )
-                    nc.scalar.copy(out=dst[:, 2 * half * P : 2 * (half + 1) * P, :], in_=il_bank[:])
-                return
-            dst_view = dst.rearrange("p (c i) t -> p c t i", i=4)
-            src_view = src[:].rearrange("p t (c i) -> p c t i", i=4)
-            if route == "V":
-                nc.vector.tensor_copy(out=dst_view, in_=src_view)
-            else:
-                nc.scalar.copy(out=dst_view, in_=src_view)
-
         def new_codes():
             codes = code_pool.tile([P, PASSES, CHUNK], U32, name="w_codes", align_bytes=64)
             scales = code_pool.tile([P, PASSES, CHUNK], U8, name="w_scales", align_bytes=64)
             return codes, scales
 
-        def quantize(grouped, cs, g):
+        def quantize(grouped, cs, pair):
+            g = 2 * pair
             nc.vector.quantize_mx(
                 out=cs[0][:, g : g + 2, :].rearrange("p g c -> p (g c)").bitcast(FP8X4),
                 scales=cs[1][:, g : g + 2, :].rearrange("p g c -> p (g c)"),
                 in_=grouped[:].rearrange("p g c t -> p (g c t)"),
             )
 
-        def project_and_rotate(cs, out_dram, blk, fine):
-            prod = epi_pool.tile([P, BATCH, 2, CHUNK_HEADS, 2, HALF], F32, name="prod", tag="prod")
+        def scalar_prepares_wq(blk, between):
+            pairs = []
+            for pair in range(2):
+                grouped = qgrp_pool.tile([P, 2, CHUNK, PACK], BF16, name="q_grouped", align_bytes=64)
+                pairs.append(grouped)
+            wides = [widen(blk, 0), widen(blk, 1)]
+            for g in range(PASSES):
+                nc.scalar.copy(out=pairs[g // 2][:, g % 2], in_=wides[g][:].rearrange("p t c -> p c t"))
+                if g == 1 and between is not None:
+                    between()
+                if g + 2 < PASSES:
+                    wides.append(widen(blk, g + 2))
+            return pairs
 
-            def add_and_store(b0, b1):
-                for u in range(2):
-                    nc.vector.tensor_tensor(
-                        out=prod[:, b0:b1, 0, :, u, :],
-                        in0=prod[:, b0:b1, 0, :, u, :],
-                        in1=prod[:, b0:b1, 1, :, 1 - u, :],
-                        op=ALU.add,
-                    )
-                for b in range(b0, b1):
-                    nc.sync.dma_start(
-                        out=out_dram[b, blk * CHUNK_HEADS : (blk + 1) * CHUNK_HEADS].rearrange("h p d -> p h d"),
-                        in_=prod[:, b, 0].rearrange("p h u d -> p h (u d)"),
-                    )
+        def vector_interleaves_wk(blk, g, pairs):
+            if g % 2 == 0:
+                grouped = kgrp_pool.tile([P, 2, CHUNK, PACK], BF16, name="k_grouped", align_bytes=64)
+                pairs.append(grouped)
+            nc.vector.tensor_copy(out=pairs[g // 2][:, g % 2], in_=wk_raw[(blk, g)][:].rearrange("p t c -> p c t"))
 
+        def project(cs):
+            accs = []
             for b in range(BATCH):
                 acc = psum.tile([P, CHUNK], F32, name="bank")
                 for g in range(PASSES):
@@ -176,31 +190,109 @@ def tile_attention_pa_kernel(tc, x, cos, sin, wq_bytes, wq_scale, wk, out_0, out
                         start=(g == 0),
                         stop=(g == PASSES - 1),
                     )
-                nc.vector.tensor_tensor(
-                    out=prod[:, b].rearrange("p r h u d -> p r (h u d)"),
-                    in0=acc[:].unsqueeze(1).to_broadcast([P, 2, CHUNK]),
-                    in1=table[:].rearrange("p r h u d -> p r (h u d)"),
-                    op=ALU.mult,
-                )
-                if fine:
-                    add_and_store(b, b + 1)
-            if not fine:
-                add_and_store(0, BATCH)
+                accs.append(acc)
+            return accs
 
-        for blk in range(BLOCKS):
-            k_cs = new_codes()
-            q_cs = new_codes()
-            for g in range(0, PASSES, 2):
-                k_grouped = new_grouped()
-                q_grouped = new_grouped()
-                for j in range(2):
-                    wide = widen(blk, g + j)
-                    interleave(WK_ROUTE[blk][g + j], wk_raw[(blk, g + j)], k_grouped[:, j])
-                    interleave(WQ_ROUTE[blk][g + j], wide, q_grouped[:, j])
-                quantize(k_grouped, k_cs, g)
-                quantize(q_grouped, q_cs, g)
-            if blk == 0:
+        def rotate(chunks, gpsimd_banks):
+            done = 0
+            for accs, out_dram, blk in chunks:
+                prod = epi_pool.tile([P, BATCH, 2, CHUNK_HEADS, 2, HALF], F32, name="prod", tag="prod")
+                rows = out_dram[:, blk * CHUNK_HEADS : (blk + 1) * CHUNK_HEADS]
+                first_v = BATCH
                 for b in range(BATCH):
-                    prepare_x(b)
-            project_and_rotate(k_cs, out_1, blk, False)
-            project_and_rotate(q_cs, out_0, blk, blk == BLOCKS - 1)
+                    nc.vector.tensor_tensor(
+                        out=prod[:, b].rearrange("p r h u d -> p r (h u d)"),
+                        in0=accs[b][:].unsqueeze(1).to_broadcast([P, 2, CHUNK]),
+                        in1=table[:].rearrange("p r h u d -> p r (h u d)"),
+                        op=ALU.mult,
+                    )
+                    if done < gpsimd_banks:
+                        for u in range(2):
+                            nc.gpsimd.tensor_tensor(
+                                out=prod[:, b, 0, :, u, :], in0=prod[:, b, 0, :, u, :], in1=prod[:, b, 1, :, 1 - u, :], op=ALU.add
+                            )
+                        nc.sync.dma_start(out=rows[b].rearrange("h p d -> p h d"), in_=prod[:, b, 0].rearrange("p h u d -> p h (u d)"))
+                    else:
+                        first_v = min(first_v, b)
+                    done += 1
+                yield_list.append((prod, rows, first_v))
+
+        def vector_adds():
+            for prod, rows, first_v in yield_list:
+                if first_v < BATCH:
+                    for u in range(2):
+                        nc.vector.tensor_tensor(
+                            out=prod[:, first_v:BATCH, 0, :, u, :],
+                            in0=prod[:, first_v:BATCH, 0, :, u, :],
+                            in1=prod[:, first_v:BATCH, 1, :, 1 - u, :],
+                            op=ALU.add,
+                        )
+                    for b in range(first_v, BATCH):
+                        nc.sync.dma_start(out=rows[b].rearrange("h p d -> p h d"), in_=prod[:, b, 0].rearrange("p h u d -> p h (u d)"))
+            yield_list.clear()
+
+        yield_list = []
+
+        x_banks = [transpose_x(b) for b in range(BATCH)]
+        xgs = []
+
+        def empty_all_x():
+            for j2 in range(2):
+                xg = xg_pool.tile([P, 2, PASSES * P * PACK], BF16, name="x_grouped", align_bytes=64)
+                xgs.append(xg)
+                for j in range(2):
+                    empty_x(x_banks[2 * j2 + j], xg, j)
+
+        q_pairs = {0: scalar_prepares_wq(0, empty_all_x)}
+        k_codes = {0: new_codes(), 1: new_codes()}
+        kp0 = []
+        kp1 = []
+        vector_interleaves_wk(0, 0, kp0)
+        vector_interleaves_wk(0, 1, kp0)
+        vector_interleaves_wk(0, 2, kp0)
+        quantize(kp0[0], k_codes[0], 0)
+        vector_interleaves_wk(0, 3, kp0)
+        vector_interleaves_wk(1, 0, kp1)
+        quantize(kp0[1], k_codes[0], 1)
+        vector_interleaves_wk(1, 1, kp1)
+        vector_interleaves_wk(1, 2, kp1)
+        quantize(kp1[0], k_codes[1], 0)
+        vector_interleaves_wk(1, 3, kp1)
+        quantize_x(xgs[0], 0)
+        quantize(kp1[1], k_codes[1], 1)
+        quantize_x(xgs[1], 2)
+        for g in range(PASSES):
+            load_wk(3, g)
+        for g in range(PASSES):
+            load_wq(3, g)
+        k_accs = {0: project(k_codes[0]), 1: project(k_codes[1])}
+        rotate([(k_accs[0], out_1, 0)], G_BANKS_OF_4)
+        vector_adds()
+
+        for i in range(BLOCKS):
+            if i + 1 < BLOCKS:
+                q_pairs[i + 1] = scalar_prepares_wq(i + 1, None)
+            q_codes = new_codes()
+            nxt = i + 2
+            if nxt < BLOCKS:
+                k_codes[nxt] = new_codes()
+                kp = []
+                vector_interleaves_wk(nxt, 0, kp)
+                vector_interleaves_wk(nxt, 1, kp)
+                quantize(q_pairs[i][0], q_codes, 0)
+                vector_interleaves_wk(nxt, 2, kp)
+                quantize(kp[0], k_codes[nxt], 0)
+                vector_interleaves_wk(nxt, 3, kp)
+                quantize(q_pairs[i][1], q_codes, 1)
+                quantize(kp[1], k_codes[nxt], 1)
+            else:
+                quantize(q_pairs[i][0], q_codes, 0)
+                quantize(q_pairs[i][1], q_codes, 1)
+            q_accs = project(q_codes)
+            if nxt < BLOCKS:
+                k_accs[nxt] = project(k_codes[nxt])
+            if i + 1 < BLOCKS:
+                rotate([(k_accs[i + 1], out_1, i + 1), (q_accs, out_0, i)], G_BANKS_OF_8)
+            else:
+                rotate([(q_accs, out_0, i)], G_BANKS_OF_4)
+            vector_adds()

@@ -24,8 +24,11 @@ BLOCKS = HEADS * HEAD_DIM // CHUNK
 
 FLOPS = 2 * BATCH * SEQ * DIM * 2 * HEADS * HEAD_DIM
 
-G_BANKS_OF_8 = 5
+G_BANKS_OF_8 = 6
 G_BANKS_OF_4 = 2
+WK_ON_SCALAR = {0: (), 1: (), 2: (), 3: ()}
+ONE_ADD = True
+WQ_ON_VECTOR = {0: (), 1: (), 2: (), 3: ()}
 
 
 def tile_attention_pa_kernel(tc, x, cos, sin, wq_bytes, wq_scale, wk, out_0, out_1):
@@ -35,7 +38,7 @@ def tile_attention_pa_kernel(tc, x, cos, sin, wq_bytes, wq_scale, wk, out_0, out
         raw_pool = ctx.enter_context(tc.tile_pool(name="raw", bufs=3))
         xg_pool = ctx.enter_context(tc.tile_pool(name="xg", bufs=2))
         wide_pool = ctx.enter_context(tc.tile_pool(name="wide", bufs=3))
-        kgrp_pool = ctx.enter_context(tc.tile_pool(name="kgrp", bufs=2))
+        kgrp_pool = ctx.enter_context(tc.tile_pool(name="kgrp", bufs=3))
         qgrp_pool = ctx.enter_context(tc.tile_pool(name="qgrp", bufs=4))
         code_pool = ctx.enter_context(tc.tile_pool(name="code", bufs=3))
         epi_pool = ctx.enter_context(tc.tile_pool(name="epi", bufs=2))
@@ -52,28 +55,33 @@ def tile_attention_pa_kernel(tc, x, cos, sin, wq_bytes, wq_scale, wk, out_0, out
             nc.sync.dma_start(out=qb[:], in_=wq_rows[g, :, :, blk * CHUNK : (blk + 1) * CHUNK])
             wq_raw[(blk, g)] = qb
 
-        def load_wk(blk, g):
+        def load_wk(blk, g, queue=None):
             kb = raw_pool.tile([P, PACK, CHUNK], BF16, name="wk_raw_%d" % g)
-            nc.sync.dma_start(out=kb[:], in_=wk_rows[g, :, :, blk * CHUNK : (blk + 1) * CHUNK])
+            (queue or nc.sync).dma_start(out=kb[:], in_=wk_rows[g, :, :, blk * CHUNK : (blk + 1) * CHUNK])
             wk_raw[(blk, g)] = kb
 
         cos_sin = keep.tile([P, 2, HALF], BF16, name="cos_sin")
+        wq_scl = keep.tile([P, PASSES, PACK], F32, name="wq_scl")
+        x_raw = epi_pool.tile([P, BATCH, DIM], BF16, name="x_raw", tag="prod")
+        load_wk(0, 0)
+        nc.sync.dma_start(out=wq_scl[:], in_=wq_scale.rearrange("(g p t) o -> p g (t o)", p=P, t=PACK))
+        load_wq(0, 0)
+        load_wk(0, 1)
+        load_wk(0, 2)
+        load_wq(0, 1)
+        load_wk(0, 3)
+        load_wq(0, 2)
+        nc.sync.dma_start(out=x_raw[:, 0, :], in_=x[0])
+        load_wk(1, 0)
+        load_wq(0, 3)
+        load_wk(1, 1)
+        nc.sync.dma_start(out=x_raw[:, 1, :], in_=x[1])
+        load_wk(1, 2)
+        nc.sync.dma_start(out=x_raw[:, 2, :], in_=x[2])
+        load_wk(1, 3)
+        nc.sync.dma_start(out=x_raw[:, 3, :], in_=x[3])
         nc.sync.dma_start(out=cos_sin[:, 0, :], in_=cos)
         nc.sync.dma_start(out=cos_sin[:, 1, :], in_=sin)
-        wq_scl = keep.tile([P, PASSES, PACK], F32, name="wq_scl")
-        nc.sync.dma_start(out=wq_scl[:], in_=wq_scale.rearrange("(g p t) o -> p g (t o)", p=P, t=PACK))
-        for g in range(PASSES):
-            load_wq(0, g)
-            load_wk(0, g)
-        x_raw = epi_pool.tile([P, BATCH, DIM], BF16, name="x_raw", tag="prod")
-        nc.sync.dma_start(out=x_raw[:, 0, :], in_=x[0])
-        nc.sync.dma_start(out=x_raw[:, 1, :], in_=x[1])
-        load_wk(1, 0)
-        nc.sync.dma_start(out=x_raw[:, 2, :], in_=x[2])
-        load_wk(1, 1)
-        nc.sync.dma_start(out=x_raw[:, 3, :], in_=x[3])
-        load_wk(1, 2)
-        load_wk(1, 3)
         for g in range(PASSES):
             load_wq(1, g)
         for g in range(PASSES):
@@ -84,23 +92,20 @@ def tile_attention_pa_kernel(tc, x, cos, sin, wq_bytes, wq_scale, wk, out_0, out
         ident = keep.tile([P, P], F32, name="ident")
         masks.make_identity(nc, ident[:])
         table = keep.tile([P, 2, CHUNK_HEADS, 2, HALF], F32, name="table")
-        nc.gpsimd.tensor_scalar(
-            out=table[:, 0].rearrange("p h u d -> p (h u) d"),
-            in0=cos_sin[:, 0, :].unsqueeze(1).to_broadcast([P, 2 * CHUNK_HEADS, HALF]),
-            scalar1=1.0,
-            scalar2=0.0,
-            op0=ALU.mult,
-            op1=ALU.add,
-        )
-        for u in range(2):
-            nc.gpsimd.tensor_scalar(
-                out=table[:, 1, :, u, :],
-                in0=cos_sin[:, 1, :].unsqueeze(1).to_broadcast([P, CHUNK_HEADS, HALF]),
-                scalar1=1.0 - 2.0 * u,
-                scalar2=0.0,
-                op0=ALU.mult,
-                op1=ALU.add,
+
+        def build_table():
+            nc.scalar.activation(
+                out=table[:, 0].rearrange("p h u d -> p (h u) d"),
+                in_=cos_sin[:, 0, :].unsqueeze(1).to_broadcast([P, 2 * CHUNK_HEADS, HALF]),
+                func=ACT.Copy,
             )
+            for u in range(2):
+                nc.scalar.activation(
+                    out=table[:, 1, :, u, :],
+                    in_=cos_sin[:, 1, :].unsqueeze(1).to_broadcast([P, CHUNK_HEADS, HALF]),
+                    func=ACT.Copy,
+                    scale=1.0 - 2.0 * u,
+                )
 
         x_codes = keep.tile([P, BATCH, PASSES * P], U32, name="x_codes", align_bytes=64)
         x_scales = keep.tile([P, BATCH, PASSES * P], U8, name="x_scales", align_bytes=64)
@@ -162,35 +167,56 @@ def tile_attention_pa_kernel(tc, x, cos, sin, wq_bytes, wq_scale, wk, out_0, out
                 pairs.append(grouped)
             wides = [widen(blk, 0), widen(blk, 1)]
             for g in range(PASSES):
-                nc.scalar.copy(out=pairs[g // 2][:, g % 2], in_=wides[g][:].rearrange("p t c -> p c t"))
+                if g in WQ_ON_VECTOR[blk]:
+                    left_to_vector.append((pairs[g // 2][:, g % 2], wides[g]))
+                else:
+                    nc.scalar.copy(
+                        out=pairs[g // 2][:, g % 2].rearrange("p (c i) t -> p c t i", i=4),
+                        in_=wides[g][:].rearrange("p t (c i) -> p c t i", i=4),
+                    )
                 if g == 1 and between is not None:
                     between()
                 if g + 2 < PASSES:
                     wides.append(widen(blk, g + 2))
             return pairs
 
+        def new_k_pair():
+            grouped = kgrp_pool.tile([P, 2, CHUNK, PACK], BF16, name="k_grouped", align_bytes=64)
+            return grouped
+
+        def scalar_interleaves_wk(blk, pairs):
+            for g in WK_ON_SCALAR[blk]:
+                nc.scalar.copy(out=pairs[g // 2][:, g % 2], in_=wk_raw[(blk, g)][:].rearrange("p t c -> p c t"))
+
         def vector_interleaves_wk(blk, g, pairs):
-            if g % 2 == 0:
-                grouped = kgrp_pool.tile([P, 2, CHUNK, PACK], BF16, name="k_grouped", align_bytes=64)
-                pairs.append(grouped)
+            if g in WK_ON_SCALAR[blk]:
+                return
             nc.vector.tensor_copy(out=pairs[g // 2][:, g % 2], in_=wk_raw[(blk, g)][:].rearrange("p t c -> p c t"))
 
-        def project(cs):
+        def new_accs():
             accs = []
             for b in range(BATCH):
                 acc = psum.tile([P, CHUNK], F32, name="bank")
-                for g in range(PASSES):
-                    rows = slice(g * P, (g + 1) * P)
-                    nc.tensor.matmul_mx(
-                        out=acc[:],
-                        lhsT=x_codes[:, b, rows].bitcast(FP8X4),
-                        lhsT_scale=x_scales[:, b, rows],
-                        rhs=cs[0][:, g, :].bitcast(FP8X4),
-                        rhs_scale=cs[1][:, g, :],
-                        start=(g == 0),
-                        stop=(g == PASSES - 1),
-                    )
                 accs.append(acc)
+            return accs
+
+        def multiply(cs, acc, b, passes):
+            for g in passes:
+                rows = slice(g * P, (g + 1) * P)
+                nc.tensor.matmul_mx(
+                    out=acc[:],
+                    lhsT=x_codes[:, b, rows].bitcast(FP8X4),
+                    lhsT_scale=x_scales[:, b, rows],
+                    rhs=cs[0][:, g, :].bitcast(FP8X4),
+                    rhs_scale=cs[1][:, g, :],
+                    start=(g == 0),
+                    stop=(g == PASSES - 1),
+                )
+
+        def project(cs):
+            accs = new_accs()
+            for b in range(BATCH):
+                multiply(cs, accs[b], b, range(PASSES))
             return accs
 
         def rotate(chunks, gpsimd_banks):
@@ -207,10 +233,13 @@ def tile_attention_pa_kernel(tc, x, cos, sin, wq_bytes, wq_scale, wk, out_0, out
                         op=ALU.mult,
                     )
                     if done < gpsimd_banks:
-                        for u in range(2):
-                            nc.gpsimd.tensor_tensor(
-                                out=prod[:, b, 0, :, u, :], in0=prod[:, b, 0, :, u, :], in1=prod[:, b, 1, :, 1 - u, :], op=ALU.add
-                            )
+                        if ONE_ADD:
+                            nc.gpsimd.tensor_tensor(out=prod[:, b, 0], in0=prod[:, b, 0], in1=prod[:, b, 1, :, ::-1, :], op=ALU.add)
+                        else:
+                            for u in range(2):
+                                nc.gpsimd.tensor_tensor(
+                                    out=prod[:, b, 0, :, u, :], in0=prod[:, b, 0, :, u, :], in1=prod[:, b, 1, :, 1 - u, :], op=ALU.add
+                                )
                         nc.sync.dma_start(out=rows[b].rearrange("h p d -> p h d"), in_=prod[:, b, 0].rearrange("p h u d -> p h (u d)"))
                     else:
                         first_v = min(first_v, b)
@@ -232,6 +261,12 @@ def tile_attention_pa_kernel(tc, x, cos, sin, wq_bytes, wq_scale, wk, out_0, out
             yield_list.clear()
 
         yield_list = []
+        left_to_vector = []
+
+        def vector_interleaves_wq():
+            for dst, wide in left_to_vector:
+                nc.vector.tensor_copy(out=dst, in_=wide[:].rearrange("p t c -> p c t"))
+            left_to_vector.clear()
 
         x_banks = [transpose_x(b) for b in range(BATCH)]
         xgs = []
@@ -242,19 +277,21 @@ def tile_attention_pa_kernel(tc, x, cos, sin, wq_bytes, wq_scale, wk, out_0, out
                 xgs.append(xg)
                 for j in range(2):
                     empty_x(x_banks[2 * j2 + j], xg, j)
+            build_table()
 
         q_pairs = {0: scalar_prepares_wq(0, empty_all_x)}
         k_codes = {0: new_codes(), 1: new_codes()}
-        kp0 = []
-        kp1 = []
+        kp0 = [new_k_pair(), new_k_pair()]
         vector_interleaves_wk(0, 0, kp0)
         vector_interleaves_wk(0, 1, kp0)
         vector_interleaves_wk(0, 2, kp0)
         quantize(kp0[0], k_codes[0], 0)
         vector_interleaves_wk(0, 3, kp0)
+        kp1 = [new_k_pair()]
         vector_interleaves_wk(1, 0, kp1)
         quantize(kp0[1], k_codes[0], 1)
         vector_interleaves_wk(1, 1, kp1)
+        kp1.append(new_k_pair())
         vector_interleaves_wk(1, 2, kp1)
         quantize(kp1[0], k_codes[1], 0)
         vector_interleaves_wk(1, 3, kp1)
@@ -265,18 +302,21 @@ def tile_attention_pa_kernel(tc, x, cos, sin, wq_bytes, wq_scale, wk, out_0, out
             load_wk(3, g)
         for g in range(PASSES):
             load_wq(3, g)
+        k_pairs = {2: [new_k_pair(), new_k_pair()]}
+        scalar_interleaves_wk(2, k_pairs[2])
         k_accs = {0: project(k_codes[0]), 1: project(k_codes[1])}
         rotate([(k_accs[0], out_1, 0)], G_BANKS_OF_4)
         vector_adds()
 
         for i in range(BLOCKS):
+            vector_interleaves_wq()
             if i + 1 < BLOCKS:
                 q_pairs[i + 1] = scalar_prepares_wq(i + 1, None)
             q_codes = new_codes()
             nxt = i + 2
             if nxt < BLOCKS:
                 k_codes[nxt] = new_codes()
-                kp = []
+                kp = k_pairs[nxt]
                 vector_interleaves_wk(nxt, 0, kp)
                 vector_interleaves_wk(nxt, 1, kp)
                 quantize(q_pairs[i][0], q_codes, 0)
@@ -285,12 +325,21 @@ def tile_attention_pa_kernel(tc, x, cos, sin, wq_bytes, wq_scale, wk, out_0, out
                 vector_interleaves_wk(nxt, 3, kp)
                 quantize(q_pairs[i][1], q_codes, 1)
                 quantize(kp[1], k_codes[nxt], 1)
-            else:
-                quantize(q_pairs[i][0], q_codes, 0)
-                quantize(q_pairs[i][1], q_codes, 1)
-            q_accs = project(q_codes)
-            if nxt < BLOCKS:
+                if nxt + 1 < BLOCKS:
+                    k_pairs[nxt + 1] = [new_k_pair(), new_k_pair()]
+                    scalar_interleaves_wk(nxt + 1, k_pairs[nxt + 1])
+                q_accs = project(q_codes)
                 k_accs[nxt] = project(k_codes[nxt])
+            else:
+                q_accs = new_accs()
+                quantize(q_pairs[i][0], q_codes, 0)
+                for b in range(2):
+                    multiply(q_codes, q_accs[b], b, (0, 1))
+                quantize(q_pairs[i][1], q_codes, 1)
+                for b in range(2):
+                    multiply(q_codes, q_accs[b], b, (2, 3))
+                for b in range(2, BATCH):
+                    multiply(q_codes, q_accs[b], b, range(PASSES))
             if i + 1 < BLOCKS:
                 rotate([(k_accs[i + 1], out_1, i + 1), (q_accs, out_0, i)], G_BANKS_OF_8)
             else:

@@ -191,7 +191,10 @@ def tile_attention_pa_kernel(tc, x, cos, sin, wq_bytes, wq_scale, wk, out_0, out
         def vector_interleaves_wk(blk, g, pairs):
             if g in WK_ON_SCALAR[blk]:
                 return
-            nc.vector.tensor_copy(out=pairs[g // 2][:, g % 2], in_=wk_raw[(blk, g)][:].rearrange("p t c -> p c t"))
+            nc.vector.tensor_copy(
+                out=pairs[g // 2][:, g % 2].rearrange("p (c i) t -> p c t i", i=4),
+                in_=wk_raw[(blk, g)][:].rearrange("p t (c i) -> p c t i", i=4),
+            )
 
         def new_accs():
             accs = []

@@ -70,10 +70,9 @@ def tile_attention_pa_kernel(tc, x, cos, sin, wq_bytes, wq_scale, wk, out_0, out
         load_wk(0, 2)
         load_wq(0, 1)
         load_wk(0, 3)
+        load_wk(1, 0)
         load_wq(0, 2)
         nc.sync.dma_start(out=x_raw[:, 0, :], in_=x[0])
-        load_wk(1, 0)
-        load_wq(0, 3)
         load_wk(1, 1)
         nc.sync.dma_start(out=x_raw[:, 1, :], in_=x[1])
         load_wk(1, 2)
@@ -82,6 +81,7 @@ def tile_attention_pa_kernel(tc, x, cos, sin, wq_bytes, wq_scale, wk, out_0, out
         nc.sync.dma_start(out=x_raw[:, 3, :], in_=x[3])
         nc.sync.dma_start(out=cos_sin[:, 0, :], in_=cos)
         nc.sync.dma_start(out=cos_sin[:, 1, :], in_=sin)
+        load_wq(0, 3)
         for g in range(PASSES):
             load_wq(1, g)
         for g in range(PASSES):
@@ -251,15 +251,9 @@ def tile_attention_pa_kernel(tc, x, cos, sin, wq_bytes, wq_scale, wk, out_0, out
 
         def vector_adds():
             for prod, rows, first_v in yield_list:
-                if first_v < BATCH:
-                    for u in range(2):
-                        nc.vector.tensor_tensor(
-                            out=prod[:, first_v:BATCH, 0, :, u, :],
-                            in0=prod[:, first_v:BATCH, 0, :, u, :],
-                            in1=prod[:, first_v:BATCH, 1, :, 1 - u, :],
-                            op=ALU.add,
-                        )
-                    for b in range(first_v, BATCH):
+                for b in range(first_v, BATCH):
+                    if True:
+                        nc.vector.tensor_tensor(out=prod[:, b, 0], in0=prod[:, b, 0], in1=prod[:, b, 1, :, ::-1, :], op=ALU.add)
                         nc.sync.dma_start(out=rows[b].rearrange("h p d -> p h d"), in_=prod[:, b, 0].rearrange("p h u d -> p h (u d)"))
             yield_list.clear()
 
@@ -309,7 +303,6 @@ def tile_attention_pa_kernel(tc, x, cos, sin, wq_bytes, wq_scale, wk, out_0, out
         scalar_interleaves_wk(2, k_pairs[2])
         k_accs = {0: project(k_codes[0]), 1: project(k_codes[1])}
         rotate([(k_accs[0], out_1, 0)], G_BANKS_OF_4)
-        vector_adds()
 
         for i in range(BLOCKS):
             vector_interleaves_wq()
@@ -321,6 +314,7 @@ def tile_attention_pa_kernel(tc, x, cos, sin, wq_bytes, wq_scale, wk, out_0, out
                 k_codes[nxt] = new_codes()
                 kp = k_pairs[nxt]
                 vector_interleaves_wk(nxt, 0, kp)
+                vector_adds()
                 vector_interleaves_wk(nxt, 1, kp)
                 quantize(q_pairs[i][0], q_codes, 0)
                 vector_interleaves_wk(nxt, 2, kp)
@@ -336,6 +330,7 @@ def tile_attention_pa_kernel(tc, x, cos, sin, wq_bytes, wq_scale, wk, out_0, out
             else:
                 q_accs = new_accs()
                 quantize(q_pairs[i][0], q_codes, 0)
+                vector_adds()
                 for b in range(2):
                     multiply(q_codes, q_accs[b], b, (0, 1))
                 quantize(q_pairs[i][1], q_codes, 1)
@@ -347,4 +342,4 @@ def tile_attention_pa_kernel(tc, x, cos, sin, wq_bytes, wq_scale, wk, out_0, out
                 rotate([(k_accs[i + 1], out_1, i + 1), (q_accs, out_0, i)], G_BANKS_OF_8)
             else:
                 rotate([(q_accs, out_0, i)], G_BANKS_OF_4)
-            vector_adds()
+        vector_adds()

@@ -63,6 +63,8 @@ def tile_attention_pa_kernel(tc, x, cos, sin, wq_bytes, wq_scale, wk, out_0, out
         cos_sin = keep.tile([P, 2, HALF], BF16, name="cos_sin")
         wq_scl = keep.tile([P, PASSES, PACK], F32, name="wq_scl")
         x_raw = epi_pool.tile([P, BATCH, DIM], BF16, name="x_raw", tag="prod")
+        nc.scalar.dma_start(out=cos_sin[:, 0, :], in_=cos)
+        nc.scalar.dma_start(out=cos_sin[:, 1, :], in_=sin)
         load_wk(0, 0)
         nc.sync.dma_start(out=wq_scl[:], in_=wq_scale.rearrange("(g p t) o -> p g (t o)", p=P, t=PACK))
         load_wq(0, 0)
@@ -79,8 +81,6 @@ def tile_attention_pa_kernel(tc, x, cos, sin, wq_bytes, wq_scale, wk, out_0, out
         nc.sync.dma_start(out=x_raw[:, 2, :], in_=x[2])
         load_wk(1, 3)
         nc.sync.dma_start(out=x_raw[:, 3, :], in_=x[3])
-        nc.sync.dma_start(out=cos_sin[:, 0, :], in_=cos)
-        nc.sync.dma_start(out=cos_sin[:, 1, :], in_=sin)
         load_wq(0, 3)
         for g in range(PASSES):
             load_wq(1, g)
@@ -151,6 +151,13 @@ def tile_attention_pa_kernel(tc, x, cos, sin, wq_bytes, wq_scale, wk, out_0, out
             codes = code_pool.tile([P, PASSES, CHUNK], U32, name="w_codes", align_bytes=64)
             scales = code_pool.tile([P, PASSES, CHUNK], U8, name="w_scales", align_bytes=64)
             return codes, scales
+
+        def quantize_unit(grouped, cs, g):
+            nc.vector.quantize_mx(
+                out=cs[0][:, g, :].bitcast(FP8X4),
+                scales=cs[1][:, g, :],
+                in_=grouped[:, g % 2].rearrange("p c t -> p (c t)"),
+            )
 
         def quantize(grouped, cs, pair):
             g = 2 * pair
@@ -274,8 +281,8 @@ def tile_attention_pa_kernel(tc, x, cos, sin, wq_bytes, wq_scale, wk, out_0, out
                 xgs.append(xg)
                 for j in range(2):
                     empty_x(x_banks[2 * j2 + j], xg, j)
-            build_table()
 
+        build_table()
         q_pairs = {0: scalar_prepares_wq(0, empty_all_x)}
         k_codes = {0: new_codes(), 1: new_codes()}
         kp0 = [new_k_pair(), new_k_pair()]
@@ -331,13 +338,23 @@ def tile_attention_pa_kernel(tc, x, cos, sin, wq_bytes, wq_scale, wk, out_0, out
                 q_accs = new_accs()
                 quantize(q_pairs[i][0], q_codes, 0)
                 vector_adds()
-                for b in range(2):
-                    multiply(q_codes, q_accs[b], b, (0, 1))
-                quantize(q_pairs[i][1], q_codes, 1)
-                for b in range(2):
-                    multiply(q_codes, q_accs[b], b, (2, 3))
-                for b in range(2, BATCH):
-                    multiply(q_codes, q_accs[b], b, range(PASSES))
+                if i + 1 < BLOCKS:
+                    for b in range(2):
+                        multiply(q_codes, q_accs[b], b, (0, 1))
+                    quantize(q_pairs[i][1], q_codes, 1)
+                    for b in range(2):
+                        multiply(q_codes, q_accs[b], b, (2, 3))
+                    for b in range(2, BATCH):
+                        multiply(q_codes, q_accs[b], b, range(PASSES))
+                else:
+                    for b in range(2):
+                        multiply(q_codes, q_accs[b], b, (0, 1))
+                    for g in (2, 3):
+                        quantize_unit(q_pairs[i][1], q_codes, g)
+                        for b in range(2):
+                            multiply(q_codes, q_accs[b], b, (g,))
+                    for b in range(2, BATCH):
+                        multiply(q_codes, q_accs[b], b, range(PASSES))
             if i + 1 < BLOCKS:
                 rotate([(k_accs[i + 1], out_1, i + 1), (q_accs, out_0, i)], G_BANKS_OF_8)
             else:

@@ -26,7 +26,8 @@ FLOPS = 2 * BATCH * SEQ * DIM * 2 * HEADS * HEAD_DIM
 
 G_BANKS_OF_8 = 6
 G_BANKS_OF_4 = 2
-WK_ON_SCALAR = {0: (), 1: (), 2: (), 3: ()}
+WK_ON_SCALAR = {0: (), 1: (), 2: (3,), 3: (3,)}
+WQ_ON_TENSOR = {0: (), 1: (1, 2), 2: (1, 2), 3: (1, 2)}
 ONE_ADD = True
 WQ_ON_VECTOR = {0: (), 1: (), 2: (), 3: ()}
 
@@ -91,6 +92,8 @@ def tile_attention_pa_kernel(tc, x, cos, sin, wq_bytes, wq_scale, wk, out_0, out
 
         ident = keep.tile([P, P], F32, name="ident")
         masks.make_identity(nc, ident[:])
+        ident_bf = keep.tile([P, P], BF16, name="ident_bf")
+        masks.make_identity(nc, ident_bf[:])
         table = keep.tile([P, 2, CHUNK_HEADS, 2, HALF], F32, name="table")
 
         def build_table():
@@ -174,7 +177,28 @@ def tile_attention_pa_kernel(tc, x, cos, sin, wq_bytes, wq_scale, wk, out_0, out
                 pairs.append(grouped)
             wides = [widen(blk, 0), widen(blk, 1)]
             for g in range(PASSES):
-                if g in WQ_ON_VECTOR[blk]:
+                if g in WQ_ON_TENSOR[blk]:
+                    stages = []
+                    for half in range(2):
+                        stage = psum.tile([P, 2 * CHUNK], BF16, name="bank")
+                        stages.append(stage)
+                        for j in range(2):
+                            c0 = (2 * half + j) * P
+                            nc.tensor.matmul(
+                                out=stage[:, j * CHUNK : (j + 1) * CHUNK].rearrange("p (c t) -> p t c", t=PACK),
+                                lhsT=ident_bf[:],
+                                rhs=wides[g][:, :, c0 : c0 + P],
+                                start=True,
+                                stop=True,
+                            )
+                    for half in range(2):
+                        nc.scalar.copy(
+                            out=pairs[g // 2][:, g % 2, 2 * half * P : 2 * (half + 1) * P, :]
+                            .rearrange("p c t -> p (c t)")
+                            .bitcast(F32),
+                            in_=stages[half][:].bitcast(F32),
+                        )
+                elif g in WQ_ON_VECTOR[blk]:
                     left_to_vector.append((pairs[g // 2][:, g % 2], wides[g]))
                 else:
                     nc.scalar.copy(
@@ -193,7 +217,10 @@ def tile_attention_pa_kernel(tc, x, cos, sin, wq_bytes, wq_scale, wk, out_0, out
 
         def scalar_interleaves_wk(blk, pairs):
             for g in WK_ON_SCALAR[blk]:
-                nc.scalar.copy(out=pairs[g // 2][:, g % 2], in_=wk_raw[(blk, g)][:].rearrange("p t c -> p c t"))
+                nc.scalar.copy(
+                    out=pairs[g // 2][:, g % 2].rearrange("p (c i) t -> p c t i", i=4),
+                    in_=wk_raw[(blk, g)][:].rearrange("p t (c i) -> p c t i", i=4),
+                )
 
         def vector_interleaves_wk(blk, g, pairs):
             if g in WK_ON_SCALAR[blk]:
@@ -313,7 +340,7 @@ def tile_attention_pa_kernel(tc, x, cos, sin, wq_bytes, wq_scale, wk, out_0, out
 
         for i in range(BLOCKS):
             vector_interleaves_wq()
-            if i + 1 < BLOCKS:
+            if i + 2 < BLOCKS:
                 q_pairs[i + 1] = scalar_prepares_wq(i + 1, None)
             q_codes = new_codes()
             nxt = i + 2
@@ -346,6 +373,7 @@ def tile_attention_pa_kernel(tc, x, cos, sin, wq_bytes, wq_scale, wk, out_0, out
                         multiply(q_codes, q_accs[b], b, (2, 3))
                     for b in range(2, BATCH):
                         multiply(q_codes, q_accs[b], b, range(PASSES))
+                    q_pairs[i + 1] = scalar_prepares_wq(i + 1, None)
                 else:
                     for b in range(2):
                         multiply(q_codes, q_accs[b], b, (0, 1))

@@ -26,7 +26,7 @@ FLOPS = 2 * BATCH * SEQ * DIM * 2 * HEADS * HEAD_DIM
 
 G_BANKS_OF_8 = 6
 G_BANKS_OF_4 = 2
-WK_ON_SCALAR = {0: (), 1: (), 2: (3,), 3: (3,)}
+WK_ON_SCALAR = {0: (), 1: (), 2: (3,), 3: (2, 3)}
 WQ_ON_TENSOR = {0: (), 1: (1, 2), 2: (1, 2), 3: (1, 2)}
 ONE_ADD = True
 WQ_ON_VECTOR = {0: (), 1: (), 2: (), 3: ()}
@@ -43,7 +43,8 @@ def tile_attention_pa_kernel(tc, x, cos, sin, wq_bytes, wq_scale, wk, out_0, out
         qgrp_pool = ctx.enter_context(tc.tile_pool(name="qgrp", bufs=4))
         code_pool = ctx.enter_context(tc.tile_pool(name="code", bufs=3))
         epi_pool = ctx.enter_context(tc.tile_pool(name="epi", bufs=2))
-        psum = ctx.enter_context(tc.psum_pool(name="psum", bufs=8))
+        psum_a = ctx.enter_context(tc.psum_pool(name="psum_a", bufs=4))
+        psum_b = ctx.enter_context(tc.psum_pool(name="psum_b", bufs=4))
         ctx.enter_context(tc.manual_schedule())
 
         wq_rows = wq_bytes.rearrange("(g p t) n -> g p t n", p=P, t=PACK)
@@ -76,13 +77,13 @@ def tile_attention_pa_kernel(tc, x, cos, sin, wq_bytes, wq_scale, wk, out_0, out
         load_wk(1, 0)
         load_wq(0, 2)
         nc.sync.dma_start(out=x_raw[:, 0, :], in_=x[0])
+        load_wq(0, 3)
         load_wk(1, 1)
         nc.sync.dma_start(out=x_raw[:, 1, :], in_=x[1])
         load_wk(1, 2)
         nc.sync.dma_start(out=x_raw[:, 2, :], in_=x[2])
         load_wk(1, 3)
         nc.sync.dma_start(out=x_raw[:, 3, :], in_=x[3])
-        load_wq(0, 3)
         for g in range(PASSES):
             load_wq(1, g)
         for g in range(PASSES):
@@ -117,7 +118,7 @@ def tile_attention_pa_kernel(tc, x, cos, sin, wq_bytes, wq_scale, wk, out_0, out
             words = x_raw[:, b, :].bitcast(F32)
             banks = []
             for half in range(2):
-                bank = psum.tile([P, 2, 2, P], F32, name="bank")
+                bank = (psum_a if b < 2 else psum_b).tile([P, 2, 2, P], F32, name="bank")
                 for gg in range(2):
                     g = 2 * half + gg
                     for u in range(2):
@@ -170,34 +171,40 @@ def tile_attention_pa_kernel(tc, x, cos, sin, wq_bytes, wq_scale, wk, out_0, out
                 in_=grouped[:].rearrange("p g c t -> p (g c t)"),
             )
 
-        def scalar_prepares_wq(blk, between):
+        def tensor_interleaves(wide, psum):
+            stages = []
+            for half in range(2):
+                stage = psum.tile([P, 2 * CHUNK], BF16, name="bank")
+                stages.append(stage)
+                for j in range(2):
+                    c0 = (2 * half + j) * P
+                    nc.tensor.matmul(
+                        out=stage[:, j * CHUNK : (j + 1) * CHUNK].rearrange("p (c t) -> p t c", t=PACK),
+                        lhsT=ident_bf[:],
+                        rhs=wide[:, :, c0 : c0 + P],
+                        start=True,
+                        stop=True,
+                    )
+            return stages
+
+        def scalar_empties(stages, pairs, g):
+            for half in range(2):
+                nc.scalar.copy(
+                    out=pairs[g // 2][:, g % 2, 2 * half * P : 2 * (half + 1) * P, :].rearrange("p c t -> p (c t)").bitcast(F32),
+                    in_=stages[half][:].bitcast(F32),
+                )
+
+        def scalar_prepares_wq(blk, between, psum):
             pairs = []
             for pair in range(2):
                 grouped = qgrp_pool.tile([P, 2, CHUNK, PACK], BF16, name="q_grouped", align_bytes=64)
                 pairs.append(grouped)
             wides = [widen(blk, 0), widen(blk, 1)]
             for g in range(PASSES):
+                if g == 2 and between is not None:
+                    between()
                 if g in WQ_ON_TENSOR[blk]:
-                    stages = []
-                    for half in range(2):
-                        stage = psum.tile([P, 2 * CHUNK], BF16, name="bank")
-                        stages.append(stage)
-                        for j in range(2):
-                            c0 = (2 * half + j) * P
-                            nc.tensor.matmul(
-                                out=stage[:, j * CHUNK : (j + 1) * CHUNK].rearrange("p (c t) -> p t c", t=PACK),
-                                lhsT=ident_bf[:],
-                                rhs=wides[g][:, :, c0 : c0 + P],
-                                start=True,
-                                stop=True,
-                            )
-                    for half in range(2):
-                        nc.scalar.copy(
-                            out=pairs[g // 2][:, g % 2, 2 * half * P : 2 * (half + 1) * P, :]
-                            .rearrange("p c t -> p (c t)")
-                            .bitcast(F32),
-                            in_=stages[half][:].bitcast(F32),
-                        )
+                    scalar_empties(tensor_interleaves(wides[g], psum), pairs, g)
                 elif g in WQ_ON_VECTOR[blk]:
                     left_to_vector.append((pairs[g // 2][:, g % 2], wides[g]))
                 else:
@@ -205,8 +212,6 @@ def tile_attention_pa_kernel(tc, x, cos, sin, wq_bytes, wq_scale, wk, out_0, out
                         out=pairs[g // 2][:, g % 2].rearrange("p (c i) t -> p c t i", i=4),
                         in_=wides[g][:].rearrange("p t (c i) -> p c t i", i=4),
                     )
-                if g == 1 and between is not None:
-                    between()
                 if g + 2 < PASSES:
                     wides.append(widen(blk, g + 2))
             return pairs
@@ -230,7 +235,7 @@ def tile_attention_pa_kernel(tc, x, cos, sin, wq_bytes, wq_scale, wk, out_0, out
                 in_=wk_raw[(blk, g)][:].rearrange("p t (c i) -> p c t i", i=4),
             )
 
-        def new_accs():
+        def new_accs(psum):
             accs = []
             for b in range(BATCH):
                 acc = psum.tile([P, CHUNK], F32, name="bank")
@@ -250,8 +255,8 @@ def tile_attention_pa_kernel(tc, x, cos, sin, wq_bytes, wq_scale, wk, out_0, out
                     stop=(g == PASSES - 1),
                 )
 
-        def project(cs):
-            accs = new_accs()
+        def project(cs, psum):
+            accs = new_accs(psum)
             for b in range(BATCH):
                 multiply(cs, accs[b], b, range(PASSES))
             return accs
@@ -299,7 +304,7 @@ def tile_attention_pa_kernel(tc, x, cos, sin, wq_bytes, wq_scale, wk, out_0, out
                 nc.vector.tensor_copy(out=dst, in_=wide[:].rearrange("p t c -> p c t"))
             left_to_vector.clear()
 
-        x_banks = [transpose_x(b) for b in range(BATCH)]
+        x_banks = {}
         xgs = []
 
         def empty_all_x():
@@ -310,7 +315,24 @@ def tile_attention_pa_kernel(tc, x, cos, sin, wq_bytes, wq_scale, wk, out_0, out
                     empty_x(x_banks[2 * j2 + j], xg, j)
 
         build_table()
-        q_pairs = {0: scalar_prepares_wq(0, empty_all_x)}
+        head_pairs = []
+        for pair in range(2):
+            grouped = qgrp_pool.tile([P, 2, CHUNK, PACK], BF16, name="q_grouped", align_bytes=64)
+            head_pairs.append(grouped)
+        head_wides = {0: widen(0, 0), 1: widen(0, 1)}
+        scalar_empties(tensor_interleaves(head_wides[0], psum_b), head_pairs, 0)
+        head_wides[2] = widen(0, 2)
+        scalar_empties(tensor_interleaves(head_wides[1], psum_b), head_pairs, 1)
+        head_wides[3] = widen(0, 3)
+        for b in range(BATCH):
+            x_banks[b] = transpose_x(b)
+        empty_all_x()
+        for g in (2, 3):
+            nc.scalar.copy(
+                out=head_pairs[1][:, g % 2].rearrange("p (c i) t -> p c t i", i=4),
+                in_=head_wides[g][:].rearrange("p t (c i) -> p c t i", i=4),
+            )
+        q_pairs = {0: head_pairs}
         k_codes = {0: new_codes(), 1: new_codes()}
         kp0 = [new_k_pair(), new_k_pair()]
         vector_interleaves_wk(0, 0, kp0)
@@ -335,13 +357,21 @@ def tile_attention_pa_kernel(tc, x, cos, sin, wq_bytes, wq_scale, wk, out_0, out
             load_wq(3, g)
         k_pairs = {2: [new_k_pair(), new_k_pair()]}
         scalar_interleaves_wk(2, k_pairs[2])
-        k_accs = {0: project(k_codes[0]), 1: project(k_codes[1])}
+        k_accs = {0: project(k_codes[0], psum_a), 1: project(k_codes[1], psum_b)}
         rotate([(k_accs[0], out_1, 0)], G_BANKS_OF_4)
+
+        def second_half(grouped, cs, accs):
+            def emit():
+                quantize(grouped, cs, 1)
+                for b in range(2):
+                    multiply(cs, accs[b], b, (2, 3))
+
+            return emit
 
         for i in range(BLOCKS):
             vector_interleaves_wq()
             if i + 2 < BLOCKS:
-                q_pairs[i + 1] = scalar_prepares_wq(i + 1, None)
+                q_pairs[i + 1] = scalar_prepares_wq(i + 1, None, psum_a)
             q_codes = new_codes()
             nxt = i + 2
             if nxt < BLOCKS:
@@ -359,21 +389,19 @@ def tile_attention_pa_kernel(tc, x, cos, sin, wq_bytes, wq_scale, wk, out_0, out
                 if nxt + 1 < BLOCKS:
                     k_pairs[nxt + 1] = [new_k_pair(), new_k_pair()]
                     scalar_interleaves_wk(nxt + 1, k_pairs[nxt + 1])
-                q_accs = project(q_codes)
-                k_accs[nxt] = project(k_codes[nxt])
+                q_accs = project(q_codes, psum_a)
+                k_accs[nxt] = project(k_codes[nxt], psum_b)
             else:
-                q_accs = new_accs()
+                q_accs = new_accs(psum_a)
                 quantize(q_pairs[i][0], q_codes, 0)
                 vector_adds()
                 if i + 1 < BLOCKS:
                     for b in range(2):
                         multiply(q_codes, q_accs[b], b, (0, 1))
-                    quantize(q_pairs[i][1], q_codes, 1)
-                    for b in range(2):
-                        multiply(q_codes, q_accs[b], b, (2, 3))
+                    second_half(q_pairs[i][1], q_codes, q_accs)()
                     for b in range(2, BATCH):
                         multiply(q_codes, q_accs[b], b, range(PASSES))
-                    q_pairs[i + 1] = scalar_prepares_wq(i + 1, None)
+                    q_pairs[i + 1] = scalar_prepares_wq(i + 1, None, psum_b)
                 else:
                     for b in range(2):
                         multiply(q_codes, q_accs[b], b, (0, 1))

@@ -38,7 +38,7 @@ def tile_attention_pa_kernel(tc, x, cos, sin, wq_bytes, wq_scale, wk, out_0, out
         keep = ctx.enter_context(tc.tile_pool(name="keep", bufs=1))
         raw_pool = ctx.enter_context(tc.tile_pool(name="raw", bufs=3))
         xg_pool = ctx.enter_context(tc.tile_pool(name="xg", bufs=2))
-        wide_pool = ctx.enter_context(tc.tile_pool(name="wide", bufs=3))
+        wide_pool = ctx.enter_context(tc.tile_pool(name="wide", bufs=4))
         kgrp_pool = ctx.enter_context(tc.tile_pool(name="kgrp", bufs=3))
         qgrp_pool = ctx.enter_context(tc.tile_pool(name="qgrp", bufs=4))
         code_pool = ctx.enter_context(tc.tile_pool(name="code", bufs=3))
@@ -216,6 +216,22 @@ def tile_attention_pa_kernel(tc, x, cos, sin, wq_bytes, wq_scale, wk, out_0, out
                     wides.append(widen(blk, g + 2))
             return pairs
 
+        def scalar_prepares_wq_three(blk, psum):
+            pairs = []
+            for pair in range(2):
+                grouped = qgrp_pool.tile([P, 2, CHUNK, PACK], BF16, name="q_grouped", align_bytes=64)
+                pairs.append(grouped)
+            wides = [widen(blk, 0), widen(blk, 1), widen(blk, 2)]
+            scalar_empties(tensor_interleaves(wides[0], psum), pairs, 0)
+            wides.append(widen(blk, 3))
+            scalar_empties(tensor_interleaves(wides[1], psum), pairs, 1)
+            scalar_empties(tensor_interleaves(wides[2], psum), pairs, 2)
+            nc.scalar.copy(
+                out=pairs[1][:, 1].rearrange("p (c i) t -> p c t i", i=4),
+                in_=wides[3][:].rearrange("p t (c i) -> p c t i", i=4),
+            )
+            return pairs
+
         def new_k_pair():
             grouped = kgrp_pool.tile([P, 2, CHUNK, PACK], BF16, name="k_grouped", align_bytes=64)
             return grouped
@@ -371,7 +387,7 @@ def tile_attention_pa_kernel(tc, x, cos, sin, wq_bytes, wq_scale, wk, out_0, out
         for i in range(BLOCKS):
             vector_interleaves_wq()
             if i + 2 < BLOCKS:
-                q_pairs[i + 1] = scalar_prepares_wq(i + 1, None, psum_a)
+                q_pairs[i + 1] = scalar_prepares_wq_three(i + 1, psum_a)
             q_codes = new_codes()
             nxt = i + 2
             if nxt < BLOCKS:

@@ -408,6 +408,19 @@ def tile_attention_pa_kernel(tc, x, cos, sin, wq_bytes, wq_scale, wk, out_0, out
                 q_accs = project(q_codes, psum_a)
                 k_accs[nxt] = project(k_codes[nxt], psum_b)
             else:
+                if i + 1 < BLOCKS:
+                    last_pairs = []
+                    for pair in range(2):
+                        grouped = qgrp_pool.tile([P, 2, CHUNK, PACK], BF16, name="q_grouped", align_bytes=64)
+                        last_pairs.append(grouped)
+                    last_wides = [widen(i + 1, 0), widen(i + 1, 1)]
+                    early_stages = tensor_interleaves(last_wides[1], psum_a)
+                    nc.scalar.copy(
+                        out=last_pairs[0][:, 0].rearrange("p (c i) t -> p c t i", i=4),
+                        in_=last_wides[0][:].rearrange("p t (c i) -> p c t i", i=4),
+                    )
+                    last_wides.append(widen(i + 1, 2))
+                    scalar_empties(early_stages, last_pairs, 1)
                 q_accs = new_accs(psum_a)
                 quantize(q_pairs[i][0], q_codes, 0)
                 vector_adds()
@@ -417,7 +430,13 @@ def tile_attention_pa_kernel(tc, x, cos, sin, wq_bytes, wq_scale, wk, out_0, out
                     second_half(q_pairs[i][1], q_codes, q_accs)()
                     for b in range(2, BATCH):
                         multiply(q_codes, q_accs[b], b, range(PASSES))
-                    q_pairs[i + 1] = scalar_prepares_wq(i + 1, None, psum_b)
+                    last_wides.append(widen(i + 1, 3))
+                    scalar_empties(tensor_interleaves(last_wides[2], psum_b), last_pairs, 2)
+                    nc.scalar.copy(
+                        out=last_pairs[1][:, 1].rearrange("p (c i) t -> p c t i", i=4),
+                        in_=last_wides[3][:].rearrange("p t (c i) -> p c t i", i=4),
+                    )
+                    q_pairs[i + 1] = last_pairs
                 else:
                     for b in range(2):
                         multiply(q_codes, q_accs[b], b, (0, 1))

@@ -77,9 +77,9 @@ def tile_attention_pa_kernel(tc, x, cos, sin, wq_bytes, wq_scale, wk, out_0, out
         load_wk(1, 0)
         load_wq(0, 2)
         nc.sync.dma_start(out=x_raw[:, 0, :], in_=x[0])
-        load_wq(0, 3)
         load_wk(1, 1)
         nc.sync.dma_start(out=x_raw[:, 1, :], in_=x[1])
+        load_wq(0, 3)
         load_wk(1, 2)
         nc.sync.dma_start(out=x_raw[:, 2, :], in_=x[2])
         load_wk(1, 3)
@@ -323,8 +323,8 @@ def tile_attention_pa_kernel(tc, x, cos, sin, wq_bytes, wq_scale, wk, out_0, out
         x_banks = {}
         xgs = []
 
-        def empty_all_x():
-            for j2 in range(2):
+        def empty_all_x(j2):
+            if True:
                 xg = xg_pool.tile([P, 2, PASSES * P * PACK], BF16, name="x_grouped", align_bytes=64)
                 xgs.append(xg)
                 for j in range(2):
@@ -339,10 +339,11 @@ def tile_attention_pa_kernel(tc, x, cos, sin, wq_bytes, wq_scale, wk, out_0, out
         scalar_empties(tensor_interleaves(head_wides[0], psum_b), head_pairs, 0)
         head_wides[2] = widen(0, 2)
         scalar_empties(tensor_interleaves(head_wides[1], psum_b), head_pairs, 1)
-        head_wides[3] = widen(0, 3)
         for b in range(BATCH):
             x_banks[b] = transpose_x(b)
-        empty_all_x()
+        empty_all_x(0)
+        head_wides[3] = widen(0, 3)
+        empty_all_x(1)
         for g in (2, 3):
             nc.scalar.copy(
                 out=head_pairs[1][:, g % 2].rearrange("p (c i) t -> p c t i", i=4),

@@ -84,10 +84,14 @@ def tile_attention_pa_kernel(tc, x, cos, sin, wq_bytes, wq_scale, wk, out_0, out
         nc.sync.dma_start(out=x_raw[:, 2, :], in_=x[2])
         load_wk(1, 3)
         nc.sync.dma_start(out=x_raw[:, 3, :], in_=x[3])
-        for g in range(PASSES):
-            load_wq(1, g)
-        for g in range(PASSES):
-            load_wk(2, g)
+        load_wk(2, 3)
+        load_wq(1, 0)
+        load_wk(2, 0)
+        load_wq(1, 1)
+        load_wk(2, 1)
+        load_wq(1, 2)
+        load_wk(2, 2)
+        load_wq(1, 3)
         for g in range(PASSES):
             load_wq(2, g)
 

@@ -343,16 +343,19 @@ def tile_attention_pa_kernel(tc, x, cos, sin, wq_bytes, wq_scale, wk, out_0, out
         scalar_empties(tensor_interleaves(head_wides[0], psum_b), head_pairs, 0)
         head_wides[2] = widen(0, 2)
         scalar_empties(tensor_interleaves(head_wides[1], psum_b), head_pairs, 1)
-        for b in range(BATCH):
+        for b in range(2):
+            x_banks[b] = transpose_x(b)
+        stages_02 = tensor_interleaves(head_wides[2], psum_a)
+        for b in range(2, BATCH):
             x_banks[b] = transpose_x(b)
         empty_all_x(0)
         head_wides[3] = widen(0, 3)
         empty_all_x(1)
-        for g in (2, 3):
-            nc.scalar.copy(
-                out=head_pairs[1][:, g % 2].rearrange("p (c i) t -> p c t i", i=4),
-                in_=head_wides[g][:].rearrange("p t (c i) -> p c t i", i=4),
-            )
+        scalar_empties(stages_02, head_pairs, 2)
+        nc.scalar.copy(
+            out=head_pairs[1][:, 1].rearrange("p (c i) t -> p c t i", i=4),
+            in_=head_wides[3][:].rearrange("p t (c i) -> p c t i", i=4),
+        )
         q_pairs = {0: head_pairs}
         k_codes = {0: new_codes(), 1: new_codes()}
         kp0 = [new_k_pair(), new_k_pair()]

@@ -286,7 +286,6 @@ def tile_attention_pa_kernel(tc, x, cos, sin, wq_bytes, wq_scale, wk, out_0, out
             for accs, out_dram, blk in chunks:
                 prod = epi_pool.tile([P, BATCH, 2, CHUNK_HEADS, 2, HALF], F32, name="prod", tag="prod")
                 rows = out_dram[:, blk * CHUNK_HEADS : (blk + 1) * CHUNK_HEADS]
-                first_v = BATCH
                 for b in range(BATCH):
                     nc.vector.tensor_tensor(
                         out=prod[:, b].rearrange("p r h u d -> p r (h u d)"),
@@ -304,17 +303,21 @@ def tile_attention_pa_kernel(tc, x, cos, sin, wq_bytes, wq_scale, wk, out_0, out
                                 )
                         nc.sync.dma_start(out=rows[b].rearrange("h p d -> p h d"), in_=prod[:, b, 0].rearrange("p h u d -> p h (u d)"))
                     else:
-                        first_v = min(first_v, b)
+                        yield_list.append((prod, rows, b))
                     done += 1
-                yield_list.append((prod, rows, first_v))
 
-        def vector_adds():
-            for prod, rows, first_v in yield_list:
-                for b in range(first_v, BATCH):
-                    if True:
-                        nc.vector.tensor_tensor(out=prod[:, b, 0], in0=prod[:, b, 0], in1=prod[:, b, 1, :, ::-1, :], op=ALU.add)
-                        nc.sync.dma_start(out=rows[b].rearrange("h p d -> p h d"), in_=prod[:, b, 0].rearrange("p h u d -> p h (u d)"))
-            yield_list.clear()
+        def vector_adds(count=None, halves=False):
+            for n in range(len(yield_list) if count is None else count):
+                prod, rows, b = yield_list[0]
+                yield_list.remove(yield_list[0])
+                cuts = (0, CHUNK_HEADS // 2, CHUNK_HEADS) if halves and not yield_list else (0, CHUNK_HEADS)
+                for h0, h1 in zip(cuts, cuts[1:]):
+                    nc.vector.tensor_tensor(
+                        out=prod[:, b, 0, h0:h1], in0=prod[:, b, 0, h0:h1], in1=prod[:, b, 1, h0:h1, ::-1, :], op=ALU.add
+                    )
+                    nc.sync.dma_start(
+                        out=rows[b, h0:h1].rearrange("h p d -> p h d"), in_=prod[:, b, 0, h0:h1].rearrange("p h u d -> p h (u d)")
+                    )
 
         yield_list = []
         left_to_vector = []
@@ -431,8 +434,8 @@ def tile_attention_pa_kernel(tc, x, cos, sin, wq_bytes, wq_scale, wk, out_0, out
                     scalar_empties(early_stages, last_pairs, 1)
                 q_accs = new_accs(psum_a)
                 quantize(q_pairs[i][0], q_codes, 0)
-                vector_adds()
                 if i + 1 < BLOCKS:
+                    vector_adds()
                     for b in range(2):
                         multiply(q_codes, q_accs[b], b, (0, 1))
                     second_half(q_pairs[i][1], q_codes, q_accs)()
@@ -452,10 +455,11 @@ def tile_attention_pa_kernel(tc, x, cos, sin, wq_bytes, wq_scale, wk, out_0, out
                         quantize_unit(q_pairs[i][1], q_codes, g)
                         for b in range(2):
                             multiply(q_codes, q_accs[b], b, (g,))
+                        vector_adds(1)
                     for b in range(2, BATCH):
                         multiply(q_codes, q_accs[b], b, range(PASSES))
             if i + 1 < BLOCKS:
                 rotate([(k_accs[i + 1], out_1, i + 1), (q_accs, out_0, i)], G_BANKS_OF_8)
             else:
                 rotate([(q_accs, out_0, i)], G_BANKS_OF_4)
-        vector_adds()
+        vector_adds(halves=True)

@@ -307,7 +307,7 @@ def tile_attention_pa_kernel(tc, x, cos, sin, wq_bytes, wq_scale, wk, out_0, out
                     done += 1
 
         def vector_adds(count=None, halves=False):
-            for n in range(len(yield_list) if count is None else count):
+            for n in range(len(yield_list) if count is None else min(count, len(yield_list))):
                 prod, rows, b = yield_list[0]
                 yield_list.remove(yield_list[0])
                 cuts = (0, CHUNK_HEADS // 2, CHUNK_HEADS) if halves and not yield_list else (0, CHUNK_HEADS)
@@ -378,10 +378,6 @@ def tile_attention_pa_kernel(tc, x, cos, sin, wq_bytes, wq_scale, wk, out_0, out
         quantize_x(xgs[0], 0)
         quantize(kp1[1], k_codes[1], 1)
         quantize_x(xgs[1], 2)
-        for g in range(PASSES):
-            load_wk(3, g)
-        for g in range(PASSES):
-            load_wq(3, g)
         k_pairs = {2: [new_k_pair(), new_k_pair()]}
         scalar_interleaves_wk(2, k_pairs[2])
         k_accs = {0: project(k_codes[0], psum_a), 1: project(k_codes[1], psum_b)}
@@ -406,6 +402,11 @@ def tile_attention_pa_kernel(tc, x, cos, sin, wq_bytes, wq_scale, wk, out_0, out
                 kp = k_pairs[nxt]
                 vector_interleaves_wk(nxt, 0, kp)
                 vector_adds()
+                for g in range(PASSES):
+                    if i == 0:
+                        load_wk(3, g)
+                    else:
+                        load_wq(3, g)
                 vector_interleaves_wk(nxt, 1, kp)
                 quantize(q_pairs[i][0], q_codes, 0)
                 vector_interleaves_wk(nxt, 2, kp)

@@ -79,8 +79,8 @@ def tile_attention_pa_kernel(tc, x, cos, sin, wq_bytes, wq_scale, wk, out_0, out
         nc.sync.dma_start(out=x_raw[:, 0, :], in_=x[0])
         load_wk(1, 1)
         nc.sync.dma_start(out=x_raw[:, 1, :], in_=x[1])
-        load_wq(0, 3)
         load_wk(1, 2)
+        load_wq(0, 3)
         nc.sync.dma_start(out=x_raw[:, 2, :], in_=x[2])
         load_wk(1, 3)
         nc.sync.dma_start(out=x_raw[:, 3, :], in_=x[3])
@@ -92,8 +92,6 @@ def tile_attention_pa_kernel(tc, x, cos, sin, wq_bytes, wq_scale, wk, out_0, out
         load_wq(1, 2)
         load_wk(2, 2)
         load_wq(1, 3)
-        for g in range(PASSES):
-            load_wq(2, g)
 
         ident = keep.tile([P, P], F32, name="ident")
         masks.make_identity(nc, ident[:])
@@ -402,6 +400,9 @@ def tile_attention_pa_kernel(tc, x, cos, sin, wq_bytes, wq_scale, wk, out_0, out
                 kp = k_pairs[nxt]
                 vector_interleaves_wk(nxt, 0, kp)
                 vector_adds()
+                for g in range(PASSES):
+                    if i == 0:
+                        load_wq(2, g)
                 for g in range(PASSES):
                     if i == 0:
                         load_wk(3, g)

from contextlib import ExitStack

import concourse.masks as masks
import concourse.mybir as mybir

F32 = mybir.dt.float32
BF16 = mybir.dt.bfloat16
U32 = mybir.dt.uint32
U8 = mybir.dt.uint8
FP8 = mybir.dt.float8_e4m3fn
FP8X4 = mybir.dt.float8_e4m3fn_x4
ACT = mybir.ActivationFunctionType
ALU = mybir.AluOpType

BATCH, SEQ, DIM, HEADS, HEAD_DIM = 4, 128, 2048, 16, 128
HALF = HEAD_DIM // 2
P = 128
PACK = 4
K_PASS = P * PACK
PASSES = DIM // K_PASS
CHUNK = 512
CHUNK_HEADS = CHUNK // HEAD_DIM
BLOCKS = HEADS * HEAD_DIM // CHUNK

FLOPS = 2 * BATCH * SEQ * DIM * 2 * HEADS * HEAD_DIM

G_BANKS_OF_8 = 6
G_BANKS_OF_4 = 2
WK_ON_SCALAR = {0: (), 1: (), 2: (3,), 3: (2, 3)}
WQ_ON_TENSOR = {0: (), 1: (1, 2), 2: (1, 2), 3: (1, 2)}
ONE_ADD = True
WQ_ON_VECTOR = {0: (), 1: (), 2: (), 3: ()}


def tile_attention_pa_kernel(tc, x, cos, sin, wq_bytes, wq_scale, wk, out_0, out_1):
    nc = tc.nc
    with ExitStack() as ctx:
        keep = ctx.enter_context(tc.tile_pool(name="keep", bufs=1))
        raw_pool = ctx.enter_context(tc.tile_pool(name="raw", bufs=3))
        xg_pool = ctx.enter_context(tc.tile_pool(name="xg", bufs=2))
        wide_pool = ctx.enter_context(tc.tile_pool(name="wide", bufs=4))
        kgrp_pool = ctx.enter_context(tc.tile_pool(name="kgrp", bufs=3))
        qgrp_pool = ctx.enter_context(tc.tile_pool(name="qgrp", bufs=4))
        code_pool = ctx.enter_context(tc.tile_pool(name="code", bufs=3))
        epi_pool = ctx.enter_context(tc.tile_pool(name="epi", bufs=2))
        psum_a = ctx.enter_context(tc.psum_pool(name="psum_a", bufs=4))
        psum_b = ctx.enter_context(tc.psum_pool(name="psum_b", bufs=4))
        ctx.enter_context(tc.manual_schedule())

        wq_rows = wq_bytes.rearrange("(g p t) n -> g p t n", p=P, t=PACK)
        wk_rows = wk.rearrange("(g p t) n -> g p t n", p=P, t=PACK)
        wq_raw = {}
        wk_raw = {}

        def load_wq(blk, g):
            qb = raw_pool.tile([P, PACK, CHUNK], U8, name="wq_bytes_%d" % g)
            nc.sync.dma_start(out=qb[:], in_=wq_rows[g, :, :, blk * CHUNK : (blk + 1) * CHUNK])
            wq_raw[(blk, g)] = qb

        def load_wk(blk, g, queue=None):
            kb = raw_pool.tile([P, PACK, CHUNK], BF16, name="wk_raw_%d" % g)
            (queue or nc.sync).dma_start(out=kb[:], in_=wk_rows[g, :, :, blk * CHUNK : (blk + 1) * CHUNK])
            wk_raw[(blk, g)] = kb

        cos_sin = keep.tile([P, 2, HALF], BF16, name="cos_sin")
        wq_scl = keep.tile([P, PASSES, PACK], F32, name="wq_scl")
        x_raw = epi_pool.tile([P, BATCH, DIM], BF16, name="x_raw", tag="prod")
        nc.scalar.dma_start(out=cos_sin[:, 0, :], in_=cos)
        nc.scalar.dma_start(out=cos_sin[:, 1, :], in_=sin)
        load_wk(0, 0)
        nc.sync.dma_start(out=wq_scl[:], in_=wq_scale.rearrange("(g p t) o -> p g (t o)", p=P, t=PACK))
        load_wq(0, 0)
        load_wk(0, 1)
        load_wk(0, 2)
        load_wq(0, 1)
        load_wk(0, 3)
        load_wk(1, 0)
        load_wq(0, 2)
        nc.sync.dma_start(out=x_raw[:, 0, :], in_=x[0])
        load_wk(1, 1)
        nc.sync.dma_start(out=x_raw[:, 1, :], in_=x[1])
        load_wk(1, 2)
        load_wq(0, 3)
        nc.sync.dma_start(out=x_raw[:, 2, :], in_=x[2])
        load_wk(1, 3)
        nc.sync.dma_start(out=x_raw[:, 3, :], in_=x[3])
        load_wk(2, 3)
        load_wq(1, 0)
        load_wk(2, 0)
        load_wq(1, 1)
        load_wk(2, 1)
        load_wq(1, 2)
        load_wk(2, 2)
        load_wq(1, 3)

        ident = keep.tile([P, P], F32, name="ident")
        masks.make_identity(nc, ident[:])
        ident_bf = keep.tile([P, P], BF16, name="ident_bf")
        masks.make_identity(nc, ident_bf[:])
        table = keep.tile([P, 2, CHUNK_HEADS, 2, HALF], F32, name="table")

        def build_table():
            nc.scalar.activation(
                out=table[:, 0].rearrange("p h u d -> p (h u) d"),
                in_=cos_sin[:, 0, :].unsqueeze(1).to_broadcast([P, 2 * CHUNK_HEADS, HALF]),
                func=ACT.Copy,
            )
            for u in range(2):
                nc.scalar.activation(
                    out=table[:, 1, :, u, :],
                    in_=cos_sin[:, 1, :].unsqueeze(1).to_broadcast([P, CHUNK_HEADS, HALF]),
                    func=ACT.Copy,
                    scale=1.0 - 2.0 * u,
                )

        x_codes = keep.tile([P, BATCH, PASSES * P], U32, name="x_codes", align_bytes=64)
        x_scales = keep.tile([P, BATCH, PASSES * P], U8, name="x_scales", align_bytes=64)

        def transpose_x(b):
            words = x_raw[:, b, :].bitcast(F32)
            banks = []
            for half in range(2):
                bank = (psum_a if b < 2 else psum_b).tile([P, 2, 2, P], F32, name="bank")
                for gg in range(2):
                    g = 2 * half + gg
                    for u in range(2):
                        nc.tensor.transpose(bank[:, gg, u, :], words[:, 256 * g + u : 256 * (g + 1) : 2], ident[:])
                banks.append(bank)
            return banks

        def empty_x(banks, xg, j):
            xg_words = xg[:, j, :].bitcast(F32).rearrange("p (g r u) -> p g r u", g=PASSES, u=2)
            for half in range(2):
                nc.scalar.copy(
                    out=xg_words[:, 2 * half : 2 * half + 2, :, :], in_=banks[half][:].rearrange("p g u r -> p g r u")
                )

        def quantize_x(xg, b):
            nc.vector.quantize_mx(
                out=x_codes[:, b : b + 2, :].rearrange("p b c -> p (b c)").bitcast(FP8X4),
                scales=x_scales[:, b : b + 2, :].rearrange("p b c -> p (b c)"),
                in_=xg[:].rearrange("p b c -> p (b c)"),
            )

        def widen(blk, g):
            wide = wide_pool.tile([P, PACK, CHUNK], BF16, name="wq_wide")
            for t in range(PACK):
                nc.scalar.activation(
                    out=wide[:, t, :],
                    in_=wq_raw[(blk, g)][:, t, :].bitcast(FP8),
                    func=ACT.Copy,
                    scale=wq_scl[:, g, t : t + 1],
                )
            return wide

        def new_codes():
            codes = code_pool.tile([P, PASSES, CHUNK], U32, name="w_codes", align_bytes=64)
            scales = code_pool.tile([P, PASSES, CHUNK], U8, name="w_scales", align_bytes=64)
            return codes, scales

        def quantize_unit(grouped, cs, g):
            nc.vector.quantize_mx(
                out=cs[0][:, g, :].bitcast(FP8X4),
                scales=cs[1][:, g, :],
                in_=grouped[:, g % 2].rearrange("p c t -> p (c t)"),
            )

        def quantize(grouped, cs, pair):
            g = 2 * pair
            nc.vector.quantize_mx(
                out=cs[0][:, g : g + 2, :].rearrange("p g c -> p (g c)").bitcast(FP8X4),
                scales=cs[1][:, g : g + 2, :].rearrange("p g c -> p (g c)"),
                in_=grouped[:].rearrange("p g c t -> p (g c t)"),
            )

        def tensor_interleaves(wide, psum):
            stages = []
            for half in range(2):
                stage = psum.tile([P, 2 * CHUNK], BF16, name="bank")
                stages.append(stage)
                for j in range(2):
                    c0 = (2 * half + j) * P
                    nc.tensor.matmul(
                        out=stage[:, j * CHUNK : (j + 1) * CHUNK].rearrange("p (c t) -> p t c", t=PACK),
                        lhsT=ident_bf[:],
                        rhs=wide[:, :, c0 : c0 + P],
                        start=True,
                        stop=True,
                    )
            return stages

        def scalar_empties(stages, pairs, g):
            for half in range(2):
                nc.scalar.copy(
                    out=pairs[g // 2][:, g % 2, 2 * half * P : 2 * (half + 1) * P, :].rearrange("p c t -> p (c t)").bitcast(F32),
                    in_=stages[half][:].bitcast(F32),
                )

        def scalar_prepares_wq(blk, between, psum):
            pairs = []
            for pair in range(2):
                grouped = qgrp_pool.tile([P, 2, CHUNK, PACK], BF16, name="q_grouped", align_bytes=64)
                pairs.append(grouped)
            wides = [widen(blk, 0), widen(blk, 1)]
            for g in range(PASSES):
                if g == 2 and between is not None:
                    between()
                if g in WQ_ON_TENSOR[blk]:
                    scalar_empties(tensor_interleaves(wides[g], psum), pairs, g)
                elif g in WQ_ON_VECTOR[blk]:
                    left_to_vector.append((pairs[g // 2][:, g % 2], wides[g]))
                else:
                    nc.scalar.copy(
                        out=pairs[g // 2][:, g % 2].rearrange("p (c i) t -> p c t i", i=4),
                        in_=wides[g][:].rearrange("p t (c i) -> p c t i", i=4),
                    )
                if g + 2 < PASSES:
                    wides.append(widen(blk, g + 2))
            return pairs

        def scalar_prepares_wq_three(blk, psum):
            pairs = []
            for pair in range(2):
                grouped = qgrp_pool.tile([P, 2, CHUNK, PACK], BF16, name="q_grouped", align_bytes=64)
                pairs.append(grouped)
            wides = [widen(blk, 0), widen(blk, 1), widen(blk, 2)]
            scalar_empties(tensor_interleaves(wides[0], psum), pairs, 0)
            wides.append(widen(blk, 3))
            scalar_empties(tensor_interleaves(wides[1], psum), pairs, 1)
            scalar_empties(tensor_interleaves(wides[2], psum), pairs, 2)
            nc.scalar.copy(
                out=pairs[1][:, 1].rearrange("p (c i) t -> p c t i", i=4),
                in_=wides[3][:].rearrange("p t (c i) -> p c t i", i=4),
            )
            return pairs

        def new_k_pair():
            grouped = kgrp_pool.tile([P, 2, CHUNK, PACK], BF16, name="k_grouped", align_bytes=64)
            return grouped

        def scalar_interleaves_wk(blk, pairs):
            for g in WK_ON_SCALAR[blk]:
                nc.scalar.copy(
                    out=pairs[g // 2][:, g % 2].rearrange("p (c i) t -> p c t i", i=4),
                    in_=wk_raw[(blk, g)][:].rearrange("p t (c i) -> p c t i", i=4),
                )

        def vector_interleaves_wk(blk, g, pairs):
            if g in WK_ON_SCALAR[blk]:
                return
            nc.vector.tensor_copy(
                out=pairs[g // 2][:, g % 2].rearrange("p (c i) t -> p c t i", i=4),
                in_=wk_raw[(blk, g)][:].rearrange("p t (c i) -> p c t i", i=4),
            )

        def new_accs(psum):
            accs = []
            for b in range(BATCH):
                acc = psum.tile([P, CHUNK], F32, name="bank")
                accs.append(acc)
            return accs

        def multiply(cs, acc, b, passes):
            for g in passes:
                rows = slice(g * P, (g + 1) * P)
                nc.tensor.matmul_mx(
                    out=acc[:],
                    lhsT=x_codes[:, b, rows].bitcast(FP8X4),
                    lhsT_scale=x_scales[:, b, rows],
                    rhs=cs[0][:, g, :].bitcast(FP8X4),
                    rhs_scale=cs[1][:, g, :],
                    start=(g == 0),
                    stop=(g == PASSES - 1),
                )

        def project(cs, psum):
            accs = new_accs(psum)
            for b in range(BATCH):
                multiply(cs, accs[b], b, range(PASSES))
            return accs

        def rotate(chunks, gpsimd_banks):
            done = 0
            for accs, out_dram, blk in chunks:
                prod = epi_pool.tile([P, BATCH, 2, CHUNK_HEADS, 2, HALF], F32, name="prod", tag="prod")
                rows = out_dram[:, blk * CHUNK_HEADS : (blk + 1) * CHUNK_HEADS]
                for b in range(BATCH):
                    nc.vector.tensor_tensor(
                        out=prod[:, b].rearrange("p r h u d -> p r (h u d)"),
                        in0=accs[b][:].unsqueeze(1).to_broadcast([P, 2, CHUNK]),
                        in1=table[:].rearrange("p r h u d -> p r (h u d)"),
                        op=ALU.mult,
                    )
                    if done < gpsimd_banks:
                        if ONE_ADD:
                            nc.gpsimd.tensor_tensor(out=prod[:, b, 0], in0=prod[:, b, 0], in1=prod[:, b, 1, :, ::-1, :], op=ALU.add)
                        else:
                            for u in range(2):
                                nc.gpsimd.tensor_tensor(
                                    out=prod[:, b, 0, :, u, :], in0=prod[:, b, 0, :, u, :], in1=prod[:, b, 1, :, 1 - u, :], op=ALU.add
                                )
                        nc.sync.dma_start(out=rows[b].rearrange("h p d -> p h d"), in_=prod[:, b, 0].rearrange("p h u d -> p h (u d)"))
                    else:
                        yield_list.append((prod, rows, b))
                    done += 1

        def vector_adds(count=None, halves=False):
            for n in range(len(yield_list) if count is None else min(count, len(yield_list))):
                prod, rows, b = yield_list[0]
                yield_list.remove(yield_list[0])
                cuts = (0, CHUNK_HEADS // 2, CHUNK_HEADS) if halves and not yield_list else (0, CHUNK_HEADS)
                for h0, h1 in zip(cuts, cuts[1:]):
                    nc.vector.tensor_tensor(
                        out=prod[:, b, 0, h0:h1], in0=prod[:, b, 0, h0:h1], in1=prod[:, b, 1, h0:h1, ::-1, :], op=ALU.add
                    )
                    nc.sync.dma_start(
                        out=rows[b, h0:h1].rearrange("h p d -> p h d"), in_=prod[:, b, 0, h0:h1].rearrange("p h u d -> p h (u d)")
                    )

        yield_list = []
        left_to_vector = []

        def vector_interleaves_wq():
            for dst, wide in left_to_vector:
                nc.vector.tensor_copy(out=dst, in_=wide[:].rearrange("p t c -> p c t"))
            left_to_vector.clear()

        x_banks = {}
        xgs = []

        def empty_all_x(j2):
            if True:
                xg = xg_pool.tile([P, 2, PASSES * P * PACK], BF16, name="x_grouped", align_bytes=64)
                xgs.append(xg)
                for j in range(2):
                    empty_x(x_banks[2 * j2 + j], xg, j)

        build_table()
        head_pairs = []
        for pair in range(2):
            grouped = qgrp_pool.tile([P, 2, CHUNK, PACK], BF16, name="q_grouped", align_bytes=64)
            head_pairs.append(grouped)
        head_wides = {0: widen(0, 0), 1: widen(0, 1)}
        scalar_empties(tensor_interleaves(head_wides[0], psum_b), head_pairs, 0)
        head_wides[2] = widen(0, 2)
        scalar_empties(tensor_interleaves(head_wides[1], psum_b), head_pairs, 1)
        for b in range(2):
            x_banks[b] = transpose_x(b)
        stages_02 = tensor_interleaves(head_wides[2], psum_a)
        for b in range(2, BATCH):
            x_banks[b] = transpose_x(b)
        empty_all_x(0)
        head_wides[3] = widen(0, 3)
        empty_all_x(1)
        scalar_empties(stages_02, head_pairs, 2)
        nc.scalar.copy(
            out=head_pairs[1][:, 1].rearrange("p (c i) t -> p c t i", i=4),
            in_=head_wides[3][:].rearrange("p t (c i) -> p c t i", i=4),
        )
        q_pairs = {0: head_pairs}
        k_codes = {0: new_codes(), 1: new_codes()}
        kp0 = [new_k_pair(), new_k_pair()]
        vector_interleaves_wk(0, 0, kp0)
        vector_interleaves_wk(0, 1, kp0)
        vector_interleaves_wk(0, 2, kp0)
        quantize(kp0[0], k_codes[0], 0)
        vector_interleaves_wk(0, 3, kp0)
        kp1 = [new_k_pair()]
        vector_interleaves_wk(1, 0, kp1)
        quantize(kp0[1], k_codes[0], 1)
        vector_interleaves_wk(1, 1, kp1)
        kp1.append(new_k_pair())
        vector_interleaves_wk(1, 2, kp1)
        quantize(kp1[0], k_codes[1], 0)
        vector_interleaves_wk(1, 3, kp1)
        quantize_x(xgs[0], 0)
        quantize(kp1[1], k_codes[1], 1)
        quantize_x(xgs[1], 2)
        k_pairs = {2: [new_k_pair(), new_k_pair()]}
        scalar_interleaves_wk(2, k_pairs[2])
        k_accs = {0: project(k_codes[0], psum_a), 1: project(k_codes[1], psum_b)}
        rotate([(k_accs[0], out_1, 0)], G_BANKS_OF_4)

        def second_half(grouped, cs, accs):
            def emit():
                quantize(grouped, cs, 1)
                for b in range(2):
                    multiply(cs, accs[b], b, (2, 3))

            return emit

        for i in range(BLOCKS):
            vector_interleaves_wq()
            if i + 2 < BLOCKS:
                q_pairs[i + 1] = scalar_prepares_wq_three(i + 1, psum_a)
            q_codes = new_codes()
            nxt = i + 2
            if nxt < BLOCKS:
                k_codes[nxt] = new_codes()
                kp = k_pairs[nxt]
                vector_interleaves_wk(nxt, 0, kp)
                vector_adds()
                for g in range(PASSES):
                    if i == 0:
                        load_wq(2, g)
                for g in range(PASSES):
                    if i == 0:
                        load_wk(3, g)
                    else:
                        load_wq(3, g)
                vector_interleaves_wk(nxt, 1, kp)
                quantize(q_pairs[i][0], q_codes, 0)
                vector_interleaves_wk(nxt, 2, kp)
                quantize(kp[0], k_codes[nxt], 0)
                vector_interleaves_wk(nxt, 3, kp)
                quantize(q_pairs[i][1], q_codes, 1)
                quantize(kp[1], k_codes[nxt], 1)
                if nxt + 1 < BLOCKS:
                    k_pairs[nxt + 1] = [new_k_pair(), new_k_pair()]
                    scalar_interleaves_wk(nxt + 1, k_pairs[nxt + 1])
                q_accs = project(q_codes, psum_a)
                k_accs[nxt] = project(k_codes[nxt], psum_b)
            else:
                if i + 1 < BLOCKS:
                    last_pairs = []
                    for pair in range(2):
                        grouped = qgrp_pool.tile([P, 2, CHUNK, PACK], BF16, name="q_grouped", align_bytes=64)
                        last_pairs.append(grouped)
                    last_wides = [widen(i + 1, 0), widen(i + 1, 1)]
                    early_stages = tensor_interleaves(last_wides[1], psum_a)
                    nc.scalar.copy(
                        out=last_pairs[0][:, 0].rearrange("p (c i) t -> p c t i", i=4),
                        in_=last_wides[0][:].rearrange("p t (c i) -> p c t i", i=4),
                    )
                    last_wides.append(widen(i + 1, 2))
                    scalar_empties(early_stages, last_pairs, 1)
                q_accs = new_accs(psum_a)
                quantize(q_pairs[i][0], q_codes, 0)
                if i + 1 < BLOCKS:
                    vector_adds()
                    for b in range(2):
                        multiply(q_codes, q_accs[b], b, (0, 1))
                    second_half(q_pairs[i][1], q_codes, q_accs)()
                    for b in range(2, BATCH):
                        multiply(q_codes, q_accs[b], b, range(PASSES))
                    last_wides.append(widen(i + 1, 3))
                    scalar_empties(tensor_interleaves(last_wides[2], psum_b), last_pairs, 2)
                    nc.scalar.copy(
                        out=last_pairs[1][:, 1].rearrange("p (c i) t -> p c t i", i=4),
                        in_=last_wides[3][:].rearrange("p t (c i) -> p c t i", i=4),
                    )
                    q_pairs[i + 1] = last_pairs
                else:
                    for b in range(2):
                        multiply(q_codes, q_accs[b], b, (0, 1))
                    for g in (2, 3):
                        quantize_unit(q_pairs[i][1], q_codes, g)
                        for b in range(2):
                            multiply(q_codes, q_accs[b], b, (g,))
                        vector_adds(1)
                    for b in range(2, BATCH):
                        multiply(q_codes, q_accs[b], b, range(PASSES))
            if i + 1 < BLOCKS:
                rotate([(k_accs[i + 1], out_1, i + 1), (q_accs, out_0, i)], G_BANKS_OF_8)
            else:
                rotate([(q_accs, out_0, i)], G_BANKS_OF_4)
        vector_adds(halves=True)
